import numpy as np
import ml_dtypes


def mxq(x, axis, fmt="e4m3"):
    dtype, down = {"e4m3": (ml_dtypes.float8_e4m3fn, 7), "e5m2": (ml_dtypes.float8_e5m2, 14)}[fmt]
    v = np.moveaxis(np.asarray(x, np.float32).astype(ml_dtypes.bfloat16).astype(np.float64), axis, -1)
    blocks = v.reshape(v.shape[:-1] + (-1, 32))
    amax = np.abs(blocks).max(-1, keepdims=True)
    byte = np.maximum(np.where(amax > 0, np.frexp(amax)[1] - 1 + 127, 0) - down, 1)
    scale = np.exp2(byte - 127.0)
    codes = (blocks / scale).astype(np.float32).astype(dtype).astype(np.float64)
    return np.moveaxis((codes * scale).reshape(v.shape), -1, axis)


WIDE = False


def mx_kscale(k):
    if not WIDE:
        return np.ones(k)
    levels = np.array([10, -10, 5, -5, 0])
    a = np.random.permutation(np.resize(levels, k // 512 * 4)).reshape(k // 512, 4)
    idx = np.arange(k)
    return np.exp2(a[idx // 512, idx % 128 // 32])


BF16 = ml_dtypes.bfloat16


def bf(x):
    return np.asarray(x, np.float32).astype(BF16)


def f64(x):
    return np.asarray(x).astype(np.float64)


E2M1 = np.array([0.0, 0.5, 1.0, 1.5, 2.0, 3.0, 4.0, 6.0, -0.0, -0.5, -1.0, -1.5, -2.0, -3.0, -4.0, -6.0])


def pack_weight(w, fmt):
    k, n = w.shape
    w = f64(bf(w)).reshape(k // 32, 32, n)
    amax = np.abs(w).max(1)
    if fmt == "e4m3":
        byte = np.frexp(amax)[1] - 1 + 127 - 7
    else:
        mant, ex = np.frexp(amax / 6.0)
        byte = np.where(mant > 0.5, ex, ex - 1) + 127
    byte = np.clip(np.where(amax > 0, byte, 1), 1, 254)
    scaled = (w * np.exp2(127.0 - byte)[:, None, :]).reshape(k, n).astype(np.float32)
    by_word = np.ascontiguousarray(scaled.reshape(k // 512, 128, 4, n).transpose(0, 1, 3, 2))
    if fmt == "e4m3":
        words = by_word.astype(ml_dtypes.float8_e4m3fn).view(np.uint8)
    else:
        c = by_word.astype(ml_dtypes.float4_e2m1fn).view(np.uint8) & 0xF
        words = c[..., 0::2] | (c[..., 1::2] << 4)
    return np.ascontiguousarray(words), np.ascontiguousarray(byte.astype(np.uint8).reshape(k // 512, 16, n))


def unpack_weight(words, scales, fmt):
    g, p, n, _ = words.shape
    if fmt == "e4m3":
        vals = np.ascontiguousarray(words).view(ml_dtypes.float8_e4m3fn).astype(np.float64)
    else:
        nib = np.empty((g, p, n, 4), np.uint8)
        nib[..., 0::2] = words & 0xF
        nib[..., 1::2] = words >> 4
        vals = E2M1[nib]
    vals = vals * np.repeat(np.exp2(scales.astype(np.float64) - 127.0), 8, axis=1)[..., None]
    return vals.transpose(0, 1, 3, 2).reshape(g * 512, n)


B, N, D = 2, 128, 4096
FMT = "e4m3"


def setup_inputs():
    s = mx_kscale(D)
    panel_embeddings = bf(np.random.standard_normal((B, N, D)) * s)
    words, scales = pack_weight(np.random.standard_normal((D, D)) * 4.0 / D / s[:, None] / s[None, :], FMT)
    b = bf(0.5 + 0.1 * np.random.standard_normal(1))
    return {"panel_embeddings": panel_embeddings,
            "W_words": words,
            "W_scales": scales,
            "b": b}


def reference(panel_embeddings, W_words, W_scales, b):
    xq = mxq(f64(panel_embeddings), 2, "e4m3")
    xw = xq @ unpack_weight(W_words, W_scales, FMT)
    scores = (mxq(xw, 2, "e4m3") @ xq.transpose(0, 2, 1)) + f64(b)
    n = panel_embeddings.shape[1]
    mask = ~np.eye(n, dtype=bool)
    return np.where(mask, scores, np.zeros_like(scores))

@@ -1,0 +1,196 @@
+from contextlib import ExitStack
+
+import concourse.mybir as mybir
+from concourse.masks import make_identity
+
+F32 = mybir.dt.float32
+BF16 = mybir.dt.bfloat16
+I32 = mybir.dt.int32
+U32 = mybir.dt.uint32
+U8 = mybir.dt.uint8
+FP8X4 = mybir.dt.float8_e4m3fn_x4
+ALU = mybir.AluOpType
+
+P = 128
+NB = 2
+D = 4096
+K_PASS = 512
+NG = D // K_PASS
+ROUND_COLS = 1024
+NR = D // ROUND_COLS
+UNITS = ROUND_COLS // K_PASS
+
+FLOPS = 2 * NB * P * D * D + 2 * NB * P * P * D
+
+
+def tile_readingorderhead_w_kernel(tc, panel_embeddings, W_words, W_scales, b, out):
+    nc = tc.nc
+    with ExitStack() as ctx:
+        keep = ctx.enter_context(tc.tile_pool(name="keep", bufs=1))
+        work = ctx.enter_context(tc.tile_pool(name="work", bufs=4))
+        psum = ctx.enter_context(tc.psum_pool(name="psum", bufs=8))
+        ctx.enter_context(tc.manual_schedule())
+
+        planes = {}
+        for r in range(NR):
+            for h in range(2):
+                pl = keep.tile([P, ROUND_COLS], U8, name="wpl%d_%d" % (r, h), align_bytes=64)
+                nc.vector.memset(pl[:].bitcast(I32), 0)
+                planes[(r, h)] = pl
+        ident_f = keep.tile([P, P], F32, name="ident_f")
+        make_identity(nc, ident_f[:])
+        ident_b = keep.tile([P, P], BF16, name="ident_b")
+        make_identity(nc, ident_b[:])
+        bias_b = keep.tile([P, 1], BF16, name="bias_b")
+        nc.scalar.dma_start(out=bias_b[:], in_=b.partition_broadcast(P))
+
+        xv = panel_embeddings.rearrange("b i d -> i b d")
+        x_sb = []
+        for h in range(2):
+            xt_sb = keep.tile([P, NB, D // 2], BF16, name="x_sb%d" % h)
+            nc.sync.dma_start(out=xt_sb[:], in_=xv[:, :, h * (D // 2):(h + 1) * (D // 2)])
+            x_sb.append(xt_sb)
+        w_sb = {}
+        for r in range(NR):
+            c0 = r * ROUND_COLS
+            for g in range(NG):
+                if g % 4 == 0:
+                    h = g // 4
+                    for q in range(4):
+                        nc.sync.dma_start(
+                            out=planes[(r, h)][32 * q:32 * q + 16, :].bitcast(I32),
+                            in_=W_scales[4 * h:4 * h + 4, 4 * q:4 * q + 4, c0:c0 + ROUND_COLS].bitcast(I32),
+                        )
+                wt = keep.tile([P, ROUND_COLS], U32, name="w%d_%d" % (r, g), align_bytes=64)
+                nc.sync.dma_start(
+                    out=wt[:].bitcast(I32),
+                    in_=W_words[g].rearrange("p n t -> p (n t)")[:, 4 * c0:4 * (c0 + ROUND_COLS)].bitcast(I32),
+                )
+                w_sb[(r, g)] = wt
+
+        xc = []
+        xs = []
+        xg_tiles = []
+        for g in range(NG):
+            h, gl = g // 4, g % 4
+            xt = psum.tile([P, 512], F32, name="xt%d" % g, tag="bank")
+            for bb in range(NB):
+                words = x_sb[h][:, bb, :].bitcast(F32)
+                for u in range(2):
+                    nc.tensor.transpose(
+                        xt[:, (bb * 2 + u) * P:(bb * 2 + u + 1) * P],
+                        words[:, 256 * gl + u:256 * (gl + 1):2],
+                        ident_f[:],
+                    )
+            if g % 2 == 0:
+                xg = work.tile([P, 2048], BF16, name="xg%d" % (g // 2), tag="xg", align_bytes=64)
+                xg_tiles.append(xg)
+            dst = xg_tiles[g // 2][:].bitcast(F32)[:, (g % 2) * 512:(g % 2 + 1) * 512]
+            dst = dst.rearrange("p (b i u) -> p b i u", b=NB, u=2)
+            src = xt[:].rearrange("p (b u i) -> p b i u", b=NB, u=2)
+            if g % 2 == 0:
+                nc.vector.tensor_copy(out=dst, in_=src)
+            else:
+                nc.scalar.copy(out=dst, in_=src)
+                codes = keep.tile([P, 512], U32, name="xc%d" % (g // 2), align_bytes=64)
+                scl = keep.tile([P, 512], U8, name="xs%d" % (g // 2), align_bytes=64)
+                nc.vector.quantize_mx(out=codes[:].bitcast(FP8X4), scales=scl[:], in_=xg_tiles[g // 2][:])
+                xc.append(codes)
+                xs.append(scl)
+
+        def x_slice(g, bb):
+            lo = ((g % 2) * NB + bb) * P
+            return xc[g // 2][:, lo:lo + P].bitcast(FP8X4), xs[g // 2][:, lo:lo + P]
+
+        mask = keep.tile([P, P], F32, name="mask")
+        nc.vector.tensor_scalar(out=mask[:], in0=ident_f[:], scalar1=-1.0, scalar2=1.0, op0=ALU.mult, op1=ALU.add)
+        bias_f = keep.tile([P, 1], F32, name="bias_f")
+        nc.vector.tensor_copy(out=bias_f[:], in_=bias_b[:])
+
+        xwc = {}
+        xws = {}
+        sc = []
+
+        def second_stage(G, bb):
+            rhs, rhs_s = x_slice(G, bb)
+            nc.tensor.matmul_mx(
+                out=sc[bb][:, 0:P],
+                lhsT=xwc[G][:, bb * P:(bb + 1) * P].bitcast(FP8X4),
+                lhsT_scale=xws[G][:, bb * P:(bb + 1) * P],
+                rhs=rhs,
+                rhs_scale=rhs_s,
+                start=(G == 0),
+                stop=(G == NG - 1),
+            )
+
+        for r in range(NR):
+            units = [(c, bb) for c in range(UNITS) for bb in range(NB)]
+            acc = {}
+            for (c, bb) in units:
+                acc[(c, bb)] = psum.tile([P, 512], F32, name="acc%d_%d_%d" % (r, c, bb), tag="bank")
+            for g in range(NG):
+                h, kk = g // 4, g % 4
+                for (c, bb) in units:
+                    lhsT, lhsT_s = x_slice(g, bb)
+                    nc.tensor.matmul_mx(
+                        out=acc[(c, bb)][:],
+                        lhsT=lhsT,
+                        lhsT_scale=lhsT_s,
+                        rhs=w_sb[(r, g)][:, c * 512:(c + 1) * 512].bitcast(FP8X4),
+                        rhs_scale=planes[(r, h)][4 * kk:P, c * 512:(c + 1) * 512],
+                        start=(g == 0),
+                        stop=(g == NG - 1),
+                    )
+            if r == NR - 1:
+                for bb in range(NB):
+                    sc.append(psum.tile([P, 512], F32, name="sc%d" % bb, tag="bank"))
+            xwb = {}
+            for i, (c, bb) in enumerate(units):
+                t = work.tile([P, 512], BF16, name="xwb%d_%d_%d" % (r, c, bb), tag="xwb", bufs=8)
+                dst = t[:].rearrange("p (t m) -> p t m", t=4)
+                src = acc[(c, bb)][:].rearrange("p (m t) -> p t m", t=4)
+                if i % 2 == 0:
+                    nc.scalar.copy(out=dst, in_=src)
+                else:
+                    nc.vector.tensor_copy(out=dst, in_=src)
+                xwb[(c, bb)] = t
+            tp = {}
+            for (c, bb) in units:
+                t = psum.tile([P, 512], BF16, name="tp%d_%d_%d" % (r, c, bb), tag="bank")
+                for tt in range(4):
+                    nc.tensor.transpose(t[:, tt * P:(tt + 1) * P], xwb[(c, bb)][:, tt * P:(tt + 1) * P], ident_b[:])
+                tp[(c, bb)] = t
+            if r == NR - 1:
+                for G in range(NG - UNITS):
+                    for bb in range(NB):
+                        second_stage(G, bb)
+            xwg = {}
+            for c in range(UNITS):
+                xwg[c] = work.tile([P, 1024], BF16, name="xwg%d_%d" % (r, c), tag="xwg", align_bytes=64)
+            for i, (c, bb) in enumerate(units):
+                dst = xwg[c][:, bb * 512:(bb + 1) * 512].rearrange("p (i t) -> p i t", t=4)
+                src = tp[(c, bb)][:].rearrange("p (t i) -> p i t", t=4)
+                if i % 2 == 0:
+                    nc.scalar.copy(out=dst, in_=src)
+                else:
+                    nc.vector.tensor_copy(out=dst, in_=src)
+            for c in range(UNITS):
+                G = r * UNITS + c
+                xwc[G] = keep.tile([P, 256], U32, name="xwc%d" % G, align_bytes=64)
+                xws[G] = keep.tile([P, 256], U8, name="xws%d" % G, align_bytes=64)
+                nc.vector.quantize_mx(out=xwc[G][:].bitcast(FP8X4), scales=xws[G][:], in_=xwg[c][:])
+
+        for G in range(NG - UNITS, NG):
+            for bb in range(NB):
+                second_stage(G, bb)
+        res = keep.tile([P, NB * P], F32, name="res")
+        for bb in range(NB):
+            nc.vector.scalar_tensor_tensor(
+                out=res[:, bb * P:(bb + 1) * P],
+                in0=sc[bb][:, 0:P],
+                scalar=bias_f[:, 0:1],
+                in1=mask[:],
+                op0=ALU.add,
+                op1=ALU.mult,
+            )
+        nc.sync.dma_start(out=out.rearrange("b i j -> i b j"), in_=res[:].rearrange("p (b j) -> p b j", b=NB))

@@ -31,6 +31,15 @@ def tile_readingorderhead_w_kernel(tc, panel_embeddings, W_words, W_scales, b, o
         psum = ctx.enter_context(tc.psum_pool(name="psum", bufs=8))
         ctx.enter_context(tc.manual_schedule())
 
+        zeros = keep.tile([P, 512], BF16, name="zeros")
+        nc.vector.memset(zeros[:], 0.0)
+        warm = psum.tile([P, 512], F32, name="warm", tag="bank")
+
+        def keep_clock_up(n):
+            for rep in range(n):
+                nc.tensor.matmul(out=warm[:], lhsT=zeros[:, 0:P], rhs=zeros[:], start=True, stop=True)
+
+        keep_clock_up(6)
         planes = {}
         for r in range(NR):
             for h in range(2):
@@ -45,71 +54,83 @@ def tile_readingorderhead_w_kernel(tc, panel_embeddings, W_words, W_scales, b, o
         nc.scalar.dma_start(out=bias_b[:], in_=b.partition_broadcast(P))
 
         xv = panel_embeddings.rearrange("b i d -> i b d")
-        x_sb = []
-        for h in range(2):
-            xt_sb = keep.tile([P, NB, D // 2], BF16, name="x_sb%d" % h)
-            nc.sync.dma_start(out=xt_sb[:], in_=xv[:, :, h * (D // 2):(h + 1) * (D // 2)])
-            x_sb.append(xt_sb)
+        x_sb = {}
         w_sb = {}
-        for r in range(NR):
+
+        def load_x(qq):
+            t = keep.tile([P, NB, 1024], BF16, name="x_sb%d" % qq)
+            nc.sync.dma_start(out=t[:], in_=xv[:, :, qq * 1024:(qq + 1) * 1024])
+            x_sb[qq] = t
+
+        def load_scales(r, h):
             c0 = r * ROUND_COLS
+            for q in range(4):
+                nc.sync.dma_start(
+                    out=planes[(r, h)][32 * q:32 * q + 16, :].bitcast(I32),
+                    in_=W_scales[4 * h:4 * h + 4, 4 * q:4 * q + 4, c0:c0 + ROUND_COLS].bitcast(I32),
+                )
+
+        def load_w(r, g):
+            c0 = r * ROUND_COLS
+            wt = keep.tile([P, ROUND_COLS], U32, name="w%d_%d" % (r, g), align_bytes=64)
+            nc.sync.dma_start(
+                out=wt[:].bitcast(I32),
+                in_=W_words[g].rearrange("p n t -> p (n t)")[:, 4 * c0:4 * (c0 + ROUND_COLS)].bitcast(I32),
+            )
+            w_sb[(r, g)] = wt
+
+        load_x(0)
+        load_x(1)
+        load_scales(0, 0)
+        load_w(0, 0)
+        load_w(0, 1)
+        load_x(2)
+        load_w(0, 2)
+        load_w(0, 3)
+        load_x(3)
+        load_scales(0, 1)
+        for g in range(4, NG):
+            load_w(0, g)
+        for r in range(1, NR):
             for g in range(NG):
                 if g % 4 == 0:
-                    h = g // 4
-                    for q in range(4):
-                        nc.sync.dma_start(
-                            out=planes[(r, h)][32 * q:32 * q + 16, :].bitcast(I32),
-                            in_=W_scales[4 * h:4 * h + 4, 4 * q:4 * q + 4, c0:c0 + ROUND_COLS].bitcast(I32),
-                        )
-                wt = keep.tile([P, ROUND_COLS], U32, name="w%d_%d" % (r, g), align_bytes=64)
-                nc.sync.dma_start(
-                    out=wt[:].bitcast(I32),
-                    in_=W_words[g].rearrange("p n t -> p (n t)")[:, 4 * c0:4 * (c0 + ROUND_COLS)].bitcast(I32),
-                )
-                w_sb[(r, g)] = wt
+                    load_scales(r, g // 4)
+                load_w(r, g)
 
-        xc = []
-        xs = []
-        xg_tiles = []
-        for g in range(NG):
-            h, gl = g // 4, g % 4
-            xt = psum.tile([P, 512], F32, name="xt%d" % g, tag="bank")
-            for bb in range(NB):
-                words = x_sb[h][:, bb, :].bitcast(F32)
-                for u in range(2):
-                    nc.tensor.transpose(
-                        xt[:, (bb * 2 + u) * P:(bb * 2 + u + 1) * P],
-                        words[:, 256 * gl + u:256 * (gl + 1):2],
-                        ident_f[:],
-                    )
-            if g % 2 == 0:
-                xg = work.tile([P, 2048], BF16, name="xg%d" % (g // 2), tag="xg", align_bytes=64)
-                xg_tiles.append(xg)
-            dst = xg_tiles[g // 2][:].bitcast(F32)[:, (g % 2) * 512:(g % 2 + 1) * 512]
-            dst = dst.rearrange("p (b i u) -> p b i u", b=NB, u=2)
-            src = xt[:].rearrange("p (b u i) -> p b i u", b=NB, u=2)
-            if g % 2 == 0:
-                nc.vector.tensor_copy(out=dst, in_=src)
-            else:
-                nc.scalar.copy(out=dst, in_=src)
-                codes = keep.tile([P, 512], U32, name="xc%d" % (g // 2), align_bytes=64)
-                scl = keep.tile([P, 512], U8, name="xs%d" % (g // 2), align_bytes=64)
-                nc.vector.quantize_mx(out=codes[:].bitcast(FP8X4), scales=scl[:], in_=xg_tiles[g // 2][:])
-                xc.append(codes)
-                xs.append(scl)
+        xc = {}
+        xs = {}
+
+        def prepare_x(qq):
+            xg = work.tile([P, 2048], BF16, name="xg%d" % qq, tag="xg", align_bytes=64)
+            for gl in range(2):
+                xt = psum.tile([P, 512], F32, name="xt%d_%d" % (qq, gl), tag="bank")
+                for bb in range(NB):
+                    words = x_sb[qq][:, bb, :].bitcast(F32)
+                    for u in range(2):
+                        nc.tensor.transpose(
+                            xt[:, (bb * 2 + u) * P:(bb * 2 + u + 1) * P],
+                            words[:, 256 * gl + u:256 * (gl + 1):2],
+                            ident_f[:],
+                        )
+                dst = xg[:].bitcast(F32)[:, gl * 512:(gl + 1) * 512]
+                dst = dst.rearrange("p (b i u) -> p b i u", b=NB, u=2)
+                src = xt[:].rearrange("p (b u i) -> p b i u", b=NB, u=2)
+                if gl == 0:
+                    nc.vector.tensor_copy(out=dst, in_=src)
+                else:
+                    nc.scalar.copy(out=dst, in_=src)
+            xc[qq] = keep.tile([P, 512], U32, name="xc%d" % qq, align_bytes=64)
+            xs[qq] = keep.tile([P, 512], U8, name="xs%d" % qq, align_bytes=64)
+            nc.vector.quantize_mx(out=xc[qq][:].bitcast(FP8X4), scales=xs[qq][:], in_=xg[:])
 
         def x_slice(g, bb):
             lo = ((g % 2) * NB + bb) * P
             return xc[g // 2][:, lo:lo + P].bitcast(FP8X4), xs[g // 2][:, lo:lo + P]
 
-        mask = keep.tile([P, P], F32, name="mask")
-        nc.vector.tensor_scalar(out=mask[:], in0=ident_f[:], scalar1=-1.0, scalar2=1.0, op0=ALU.mult, op1=ALU.add)
-        bias_f = keep.tile([P, 1], F32, name="bias_f")
-        nc.vector.tensor_copy(out=bias_f[:], in_=bias_b[:])
-
         xwc = {}
         xws = {}
         sc = []
+        units = [(c, bb) for c in range(UNITS) for bb in range(NB)]
 
         def second_stage(G, bb):
             rhs, rhs_s = x_slice(G, bb)
@@ -123,24 +144,39 @@ def tile_readingorderhead_w_kernel(tc, panel_embeddings, W_words, W_scales, b, o
                 stop=(G == NG - 1),
             )
 
+        def first_stage(r, g, acc):
+            h, kk = g // 4, g % 4
+            for (c, bb) in units:
+                lhsT, lhsT_s = x_slice(g, bb)
+                nc.tensor.matmul_mx(
+                    out=acc[(c, bb)][:],
+                    lhsT=lhsT,
+                    lhsT_scale=lhsT_s,
+                    rhs=w_sb[(r, g)][:, c * 512:(c + 1) * 512].bitcast(FP8X4),
+                    rhs_scale=planes[(r, h)][4 * kk:P, c * 512:(c + 1) * 512],
+                    start=(g == 0),
+                    stop=(g == NG - 1),
+                )
+
+        prepare_x(0)
+        keep_clock_up(2)
+        prepare_x(1)
+        keep_clock_up(2)
+        mask = keep.tile([P, P], F32, name="mask")
+        nc.vector.tensor_scalar(out=mask[:], in0=ident_f[:], scalar1=-1.0, scalar2=1.0, op0=ALU.mult, op1=ALU.add)
+        bias_f = keep.tile([P, 1], F32, name="bias_f")
+        nc.vector.tensor_copy(out=bias_f[:], in_=bias_b[:])
+
         for r in range(NR):
-            units = [(c, bb) for c in range(UNITS) for bb in range(NB)]
             acc = {}
             for (c, bb) in units:
                 acc[(c, bb)] = psum.tile([P, 512], F32, name="acc%d_%d_%d" % (r, c, bb), tag="bank")
             for g in range(NG):
-                h, kk = g // 4, g % 4
-                for (c, bb) in units:
-                    lhsT, lhsT_s = x_slice(g, bb)
-                    nc.tensor.matmul_mx(
-                        out=acc[(c, bb)][:],
-                        lhsT=lhsT,
-                        lhsT_scale=lhsT_s,
-                        rhs=w_sb[(r, g)][:, c * 512:(c + 1) * 512].bitcast(FP8X4),
-                        rhs_scale=planes[(r, h)][4 * kk:P, c * 512:(c + 1) * 512],
-                        start=(g == 0),
-                        stop=(g == NG - 1),
-                    )
+                first_stage(r, g, acc)
+                if r == 0 and g == 1:
+                    prepare_x(2)
+                if r == 0 and g == 3:
+                    prepare_x(3)
             if r == NR - 1:
                 for bb in range(NB):
                     sc.append(psum.tile([P, 512], F32, name="sc%d" % bb, tag="bank"))

@@ -40,18 +40,39 @@ def tile_readingorderhead_w_kernel(tc, panel_embeddings, W_words, W_scales, b, o
                 nc.tensor.matmul(out=warm[:], lhsT=zeros[:, 0:P], rhs=zeros[:], start=True, stop=True)
 
         keep_clock_up(6)
-        planes = {}
-        for r in range(NR):
-            for h in range(2):
-                pl = keep.tile([P, ROUND_COLS], U8, name="wpl%d_%d" % (r, h), align_bytes=64)
-                nc.vector.memset(pl[:].bitcast(I32), 0)
-                planes[(r, h)] = pl
+        pl_first = keep.tile([P, ROUND_COLS], U8, name="pl_first", align_bytes=64)
+        nc.vector.memset(pl_first[:].bitcast(I32), 0)
+        pl_high = keep.tile([P, D], U8, name="pl_high", align_bytes=64)
+        nc.vector.memset(pl_high[:].bitcast(I32), 0)
+        pl_low = keep.tile([P, D - ROUND_COLS], U8, name="pl_low", align_bytes=64)
+        nc.vector.memset(pl_low[:].bitcast(I32), 0)
+
+        def w_plane(r, g, c):
+            kk = g % 4
+            if g >= 4:
+                lo = r * ROUND_COLS + c * 512
+                return pl_high[4 * kk:P, lo:lo + 512]
+            if r == 0:
+                return pl_first[4 * kk:P, c * 512:(c + 1) * 512]
+            lo = (r - 1) * ROUND_COLS + c * 512
+            return pl_low[4 * kk:P, lo:lo + 512]
+
         ident_f = keep.tile([P, P], F32, name="ident_f")
         make_identity(nc, ident_f[:])
         ident_b = keep.tile([P, P], BF16, name="ident_b")
         make_identity(nc, ident_b[:])
         bias_b = keep.tile([P, 1], BF16, name="bias_b")
         nc.scalar.dma_start(out=bias_b[:], in_=b.partition_broadcast(P))
+        for q in range(4):
+            nc.gpsimd.dma_start(
+                out=pl_high[32 * q:32 * q + 16, :].bitcast(F32),
+                in_=W_scales[4:8, 4 * q:4 * q + 4, :].bitcast(F32),
+            )
+        for q in range(4):
+            nc.gpsimd.dma_start(
+                out=pl_low[32 * q:32 * q + 16, :].bitcast(F32),
+                in_=W_scales[0:4, 4 * q:4 * q + 4, ROUND_COLS:D].bitcast(F32),
+            )
 
         xv = panel_embeddings.rearrange("b i d -> i b d")
         x_sb = {}
@@ -62,12 +83,11 @@ def tile_readingorderhead_w_kernel(tc, panel_embeddings, W_words, W_scales, b, o
             nc.sync.dma_start(out=t[:], in_=xv[:, :, qq * 1024:(qq + 1) * 1024])
             x_sb[qq] = t
 
-        def load_scales(r, h):
-            c0 = r * ROUND_COLS
+        def load_first_scales():
             for q in range(4):
                 nc.sync.dma_start(
-                    out=planes[(r, h)][32 * q:32 * q + 16, :].bitcast(I32),
-                    in_=W_scales[4 * h:4 * h + 4, 4 * q:4 * q + 4, c0:c0 + ROUND_COLS].bitcast(I32),
+                    out=pl_first[32 * q:32 * q + 16, :].bitcast(I32),
+                    in_=W_scales[0:4, 4 * q:4 * q + 4, 0:ROUND_COLS].bitcast(I32),
                 )
 
         def load_w(r, g):
@@ -81,20 +101,17 @@ def tile_readingorderhead_w_kernel(tc, panel_embeddings, W_words, W_scales, b, o
 
         load_x(0)
         load_x(1)
-        load_scales(0, 0)
+        load_first_scales()
         load_w(0, 0)
         load_w(0, 1)
         load_x(2)
         load_w(0, 2)
         load_w(0, 3)
         load_x(3)
-        load_scales(0, 1)
         for g in range(4, NG):
             load_w(0, g)
         for r in range(1, NR):
             for g in range(NG):
-                if g % 4 == 0:
-                    load_scales(r, g // 4)
                 load_w(r, g)
 
         xc = {}
@@ -145,7 +162,6 @@ def tile_readingorderhead_w_kernel(tc, panel_embeddings, W_words, W_scales, b, o
             )
 
         def first_stage(r, g, acc):
-            h, kk = g // 4, g % 4
             for (c, bb) in units:
                 lhsT, lhsT_s = x_slice(g, bb)
                 nc.tensor.matmul_mx(
@@ -153,7 +169,7 @@ def tile_readingorderhead_w_kernel(tc, panel_embeddings, W_words, W_scales, b, o
                     lhsT=lhsT,
                     lhsT_scale=lhsT_s,
                     rhs=w_sb[(r, g)][:, c * 512:(c + 1) * 512].bitcast(FP8X4),
-                    rhs_scale=planes[(r, h)][4 * kk:P, c * 512:(c + 1) * 512],
+                    rhs_scale=w_plane(r, g, c),
                     start=(g == 0),
                     stop=(g == NG - 1),
                 )

@@ -19,6 +19,7 @@ NG = D // K_PASS
 ROUND_COLS = 1024
 NR = D // ROUND_COLS
 UNITS = ROUND_COLS // K_PASS
+PAD_WORDS = 48
 
 FLOPS = 2 * NB * P * D * D + 2 * NB * P * P * D
 
@@ -40,39 +41,18 @@ def tile_readingorderhead_w_kernel(tc, panel_embeddings, W_words, W_scales, b, o
                 nc.tensor.matmul(out=warm[:], lhsT=zeros[:, 0:P], rhs=zeros[:], start=True, stop=True)
 
         keep_clock_up(6)
-        pl_first = keep.tile([P, ROUND_COLS], U8, name="pl_first", align_bytes=64)
-        nc.vector.memset(pl_first[:].bitcast(I32), 0)
-        pl_high = keep.tile([P, D], U8, name="pl_high", align_bytes=64)
-        nc.vector.memset(pl_high[:].bitcast(I32), 0)
-        pl_low = keep.tile([P, D - ROUND_COLS], U8, name="pl_low", align_bytes=64)
-        nc.vector.memset(pl_low[:].bitcast(I32), 0)
-
-        def w_plane(r, g, c):
-            kk = g % 4
-            if g >= 4:
-                lo = r * ROUND_COLS + c * 512
-                return pl_high[4 * kk:P, lo:lo + 512]
-            if r == 0:
-                return pl_first[4 * kk:P, c * 512:(c + 1) * 512]
-            lo = (r - 1) * ROUND_COLS + c * 512
-            return pl_low[4 * kk:P, lo:lo + 512]
-
+        planes = {}
+        for r in range(NR):
+            for h in range(2):
+                pl = keep.tile([P, ROUND_COLS], U8, name="wpl%d_%d" % (r, h), align_bytes=256)
+                nc.vector.memset(pl[:].bitcast(I32), 0)
+                planes[(r, h)] = pl
         ident_f = keep.tile([P, P], F32, name="ident_f")
         make_identity(nc, ident_f[:])
         ident_b = keep.tile([P, P], BF16, name="ident_b")
         make_identity(nc, ident_b[:])
         bias_b = keep.tile([P, 1], BF16, name="bias_b")
         nc.scalar.dma_start(out=bias_b[:], in_=b.partition_broadcast(P))
-        for q in range(4):
-            nc.gpsimd.dma_start(
-                out=pl_high[32 * q:32 * q + 16, :].bitcast(F32),
-                in_=W_scales[4:8, 4 * q:4 * q + 4, :].bitcast(F32),
-            )
-        for q in range(4):
-            nc.gpsimd.dma_start(
-                out=pl_low[32 * q:32 * q + 16, :].bitcast(F32),
-                in_=W_scales[0:4, 4 * q:4 * q + 4, ROUND_COLS:D].bitcast(F32),
-            )
 
         xv = panel_embeddings.rearrange("b i d -> i b d")
         x_sb = {}
@@ -83,16 +63,17 @@ def tile_readingorderhead_w_kernel(tc, panel_embeddings, W_words, W_scales, b, o
             nc.sync.dma_start(out=t[:], in_=xv[:, :, qq * 1024:(qq + 1) * 1024])
             x_sb[qq] = t
 
-        def load_first_scales():
+        def load_scales(r, h):
+            c0 = r * ROUND_COLS
             for q in range(4):
                 nc.sync.dma_start(
-                    out=pl_first[32 * q:32 * q + 16, :].bitcast(I32),
-                    in_=W_scales[0:4, 4 * q:4 * q + 4, 0:ROUND_COLS].bitcast(I32),
+                    out=planes[(r, h)][32 * q:32 * q + 16, :].bitcast(I32),
+                    in_=W_scales[4 * h:4 * h + 4, 4 * q:4 * q + 4, c0:c0 + ROUND_COLS].bitcast(I32),
                 )
 
         def load_w(r, g):
             c0 = r * ROUND_COLS
-            wt = keep.tile([P, ROUND_COLS], U32, name="w%d_%d" % (r, g), align_bytes=64)
+            wt = keep.tile([P, ROUND_COLS], U32, name="w%d_%d" % (r, g), align_bytes=256)
             nc.sync.dma_start(
                 out=wt[:].bitcast(I32),
                 in_=W_words[g].rearrange("p n t -> p (n t)")[:, 4 * c0:4 * (c0 + ROUND_COLS)].bitcast(I32),
@@ -101,17 +82,20 @@ def tile_readingorderhead_w_kernel(tc, panel_embeddings, W_words, W_scales, b, o
 
         load_x(0)
         load_x(1)
-        load_first_scales()
+        load_scales(0, 0)
         load_w(0, 0)
         load_w(0, 1)
         load_x(2)
         load_w(0, 2)
         load_w(0, 3)
         load_x(3)
+        load_scales(0, 1)
         for g in range(4, NG):
             load_w(0, g)
         for r in range(1, NR):
             for g in range(NG):
+                if g % 4 == 0:
+                    load_scales(r, g // 4)
                 load_w(r, g)
 
         xc = {}
@@ -119,6 +103,8 @@ def tile_readingorderhead_w_kernel(tc, panel_embeddings, W_words, W_scales, b, o
 
         def prepare_x(qq):
             xg = work.tile([P, 2048], BF16, name="xg%d" % qq, tag="xg", align_bytes=64)
+            xc[qq] = keep.tile([P, PAD_WORDS + 512], U32, name="xc%d" % qq, align_bytes=256)
+            xs[qq] = keep.tile([P, 4 * 256], U8, name="xs%d" % qq, align_bytes=256)
             for gl in range(2):
                 xt = psum.tile([P, 512], F32, name="xt%d_%d" % (qq, gl), tag="bank")
                 for bb in range(NB):
@@ -136,13 +122,20 @@ def tile_readingorderhead_w_kernel(tc, panel_embeddings, W_words, W_scales, b, o
                     nc.vector.tensor_copy(out=dst, in_=src)
                 else:
                     nc.scalar.copy(out=dst, in_=src)
-            xc[qq] = keep.tile([P, 512], U32, name="xc%d" % qq, align_bytes=64)
-            xs[qq] = keep.tile([P, 512], U8, name="xs%d" % qq, align_bytes=64)
-            nc.vector.quantize_mx(out=xc[qq][:].bitcast(FP8X4), scales=xs[qq][:], in_=xg[:])
+                for bb in range(NB):
+                    j = gl * NB + bb
+                    nc.vector.quantize_mx(
+                        out=xc[qq][:, PAD_WORDS + j * P:PAD_WORDS + (j + 1) * P].bitcast(FP8X4),
+                        scales=xs[qq][:, j * 256:j * 256 + P],
+                        in_=xg[:, j * 512:(j + 1) * 512],
+                    )
 
         def x_slice(g, bb):
-            lo = ((g % 2) * NB + bb) * P
-            return xc[g // 2][:, lo:lo + P].bitcast(FP8X4), xs[g // 2][:, lo:lo + P]
+            j = (g % 2) * NB + bb
+            return (
+                xc[g // 2][:, PAD_WORDS + j * P:PAD_WORDS + (j + 1) * P].bitcast(FP8X4),
+                xs[g // 2][:, j * 256:j * 256 + P],
+            )
 
         xwc = {}
         xws = {}
@@ -162,6 +155,7 @@ def tile_readingorderhead_w_kernel(tc, panel_embeddings, W_words, W_scales, b, o
             )
 
         def first_stage(r, g, acc):
+            h, kk = g // 4, g % 4
             for (c, bb) in units:
                 lhsT, lhsT_s = x_slice(g, bb)
                 nc.tensor.matmul_mx(
@@ -169,7 +163,7 @@ def tile_readingorderhead_w_kernel(tc, panel_embeddings, W_words, W_scales, b, o
                     lhsT=lhsT,
                     lhsT_scale=lhsT_s,
                     rhs=w_sb[(r, g)][:, c * 512:(c + 1) * 512].bitcast(FP8X4),
-                    rhs_scale=w_plane(r, g, c),
+                    rhs_scale=planes[(r, h)][4 * kk:P, c * 512:(c + 1) * 512],
                     start=(g == 0),
                     stop=(g == NG - 1),
                 )

@@ -71,32 +71,42 @@ def tile_readingorderhead_w_kernel(tc, panel_embeddings, W_words, W_scales, b, o
                     in_=W_scales[4 * h:4 * h + 4, 4 * q:4 * q + 4, c0:c0 + ROUND_COLS].bitcast(I32),
                 )
 
-        def load_w(r, g):
-            c0 = r * ROUND_COLS
-            wt = keep.tile([P, ROUND_COLS], U32, name="w%d_%d" % (r, g), align_bytes=256)
+        def load_w(r, g, halves):
+            c0 = r * ROUND_COLS + halves[0] * 512
+            n = len(halves) * 512
+            wt = keep.tile([P, n], U32, name="w%d_%d_%d" % (r, g, halves[0]), align_bytes=256)
             nc.sync.dma_start(
                 out=wt[:].bitcast(I32),
-                in_=W_words[g].rearrange("p n t -> p (n t)")[:, 4 * c0:4 * (c0 + ROUND_COLS)].bitcast(I32),
+                in_=W_words[g].rearrange("p n t -> p (n t)")[:, 4 * c0:4 * (c0 + n)].bitcast(I32),
             )
-            w_sb[(r, g)] = wt
+            for i, c in enumerate(halves):
+                w_sb[(r, g, c)] = wt[:, i * 512:(i + 1) * 512]
 
+        LAST = NR - 1
         load_x(0)
         load_x(1)
         load_scales(0, 0)
-        load_w(0, 0)
-        load_w(0, 1)
+        load_w(0, 0, [0, 1])
+        load_w(0, 1, [0, 1])
         load_x(2)
-        load_w(0, 2)
-        load_w(0, 3)
+        load_w(0, 2, [0, 1])
+        load_w(0, 3, [0, 1])
         load_x(3)
         load_scales(0, 1)
         for g in range(4, NG):
-            load_w(0, g)
-        for r in range(1, NR):
+            load_w(0, g, [0, 1])
+        for r in range(1, LAST):
             for g in range(NG):
                 if g % 4 == 0:
                     load_scales(r, g // 4)
-                load_w(r, g)
+                load_w(r, g, [0, 1])
+        load_scales(LAST, 0)
+        for g in range(4):
+            load_w(LAST, g, [0, 1])
+        load_scales(LAST, 1)
+        for c in range(UNITS):
+            for g in range(4, NG):
+                load_w(LAST, g, [c])
 
         xc = {}
         xs = {}
@@ -137,36 +147,78 @@ def tile_readingorderhead_w_kernel(tc, panel_embeddings, W_words, W_scales, b, o
                 xs[g // 2][:, j * 256:j * 256 + P],
             )
 
+        acc = {}
+        xwb = {}
+        tp = {}
+        xwg = {}
         xwc = {}
         xws = {}
         sc = []
         units = [(c, bb) for c in range(UNITS) for bb in range(NB)]
 
+        def first_stage(r, g, which):
+            h, kk = g // 4, g % 4
+            for (c, bb) in which:
+                lhsT, lhsT_s = x_slice(g, bb)
+                nc.tensor.matmul_mx(
+                    out=acc[(r, c, bb)][:],
+                    lhsT=lhsT,
+                    lhsT_scale=lhsT_s,
+                    rhs=w_sb[(r, g, c)].bitcast(FP8X4),
+                    rhs_scale=planes[(r, h)][4 * kk:P, c * 512:(c + 1) * 512],
+                    start=(g == 0),
+                    stop=(g == NG - 1),
+                )
+
+        def copy_on(on_vector, dst, src):
+            if on_vector:
+                nc.vector.tensor_copy(out=dst, in_=src)
+            else:
+                nc.scalar.copy(out=dst, in_=src)
+
+        def leave_bank(r, c, bb, on_vector):
+            t = work.tile([P, 512], BF16, name="xwb%d_%d_%d" % (r, c, bb), tag="xwb", bufs=8)
+            copy_on(
+                on_vector,
+                t[:].rearrange("p (t m) -> p t m", t=4),
+                acc[(r, c, bb)][:].rearrange("p (m t) -> p t m", t=4),
+            )
+            xwb[(r, c, bb)] = t
+
+        def transpose_unit(r, c, bb):
+            t = psum.tile([P, 512], BF16, name="tp%d_%d_%d" % (r, c, bb), tag="bank")
+            for tt in range(4):
+                nc.tensor.transpose(t[:, tt * P:(tt + 1) * P], xwb[(r, c, bb)][:, tt * P:(tt + 1) * P], ident_b[:])
+            tp[(r, c, bb)] = t
+
+        def regroup_unit(r, c, bb, on_vector):
+            t = work.tile([P, 512], BF16, name="xwg%d_%d_%d" % (r, c, bb), tag="xwg", bufs=8, align_bytes=64)
+            copy_on(
+                on_vector,
+                t[:].rearrange("p (i t) -> p i t", t=4),
+                tp[(r, c, bb)][:].rearrange("p (t i) -> p i t", t=4),
+            )
+            xwg[(r, c, bb)] = t
+
+        def quantise_unit(r, c, bb):
+            G = r * UNITS + c
+            xwc[(G, bb)] = keep.tile([P, P], U32, name="xwc%d_%d" % (G, bb), align_bytes=64)
+            xws[(G, bb)] = keep.tile([P, P], U8, name="xws%d_%d" % (G, bb), align_bytes=64)
+            nc.vector.quantize_mx(
+                out=xwc[(G, bb)][:].bitcast(FP8X4), scales=xws[(G, bb)][:], in_=xwg[(r, c, bb)][:]
+            )
+
         def second_stage(G, bb):
             rhs, rhs_s = x_slice(G, bb)
             nc.tensor.matmul_mx(
                 out=sc[bb][:, 0:P],
-                lhsT=xwc[G][:, bb * P:(bb + 1) * P].bitcast(FP8X4),
-                lhsT_scale=xws[G][:, bb * P:(bb + 1) * P],
+                lhsT=xwc[(G, bb)][:].bitcast(FP8X4),
+                lhsT_scale=xws[(G, bb)][:],
                 rhs=rhs,
                 rhs_scale=rhs_s,
                 start=(G == 0),
                 stop=(G == NG - 1),
             )
-
-        def first_stage(r, g, acc):
-            h, kk = g // 4, g % 4
-            for (c, bb) in units:
-                lhsT, lhsT_s = x_slice(g, bb)
-                nc.tensor.matmul_mx(
-                    out=acc[(c, bb)][:],
-                    lhsT=lhsT,
-                    lhsT_scale=lhsT_s,
-                    rhs=w_sb[(r, g)][:, c * 512:(c + 1) * 512].bitcast(FP8X4),
-                    rhs_scale=planes[(r, h)][4 * kk:P, c * 512:(c + 1) * 512],
-                    start=(g == 0),
-                    stop=(g == NG - 1),
-                )
 
         prepare_x(0)
         keep_clock_up(2)
@@ -177,59 +229,61 @@ def tile_readingorderhead_w_kernel(tc, panel_embeddings, W_words, W_scales, b, o
         bias_f = keep.tile([P, 1], F32, name="bias_f")
         nc.vector.tensor_copy(out=bias_f[:], in_=bias_b[:])
 
-        for r in range(NR):
-            acc = {}
+        for r in range(LAST):
             for (c, bb) in units:
-                acc[(c, bb)] = psum.tile([P, 512], F32, name="acc%d_%d_%d" % (r, c, bb), tag="bank")
+                acc[(r, c, bb)] = psum.tile([P, 512], F32, name="acc%d_%d_%d" % (r, c, bb), tag="bank")
             for g in range(NG):
-                first_stage(r, g, acc)
+                first_stage(r, g, units)
                 if r == 0 and g == 1:
                     prepare_x(2)
                 if r == 0 and g == 3:
                     prepare_x(3)
-            if r == NR - 1:
-                for bb in range(NB):
-                    sc.append(psum.tile([P, 512], F32, name="sc%d" % bb, tag="bank"))
-            xwb = {}
             for i, (c, bb) in enumerate(units):
-                t = work.tile([P, 512], BF16, name="xwb%d_%d_%d" % (r, c, bb), tag="xwb", bufs=8)
-                dst = t[:].rearrange("p (t m) -> p t m", t=4)
-                src = acc[(c, bb)][:].rearrange("p (m t) -> p t m", t=4)
-                if i % 2 == 0:
-                    nc.scalar.copy(out=dst, in_=src)
-                else:
-                    nc.vector.tensor_copy(out=dst, in_=src)
-                xwb[(c, bb)] = t
-            tp = {}
+                leave_bank(r, c, bb, i % 2 == 1)
             for (c, bb) in units:
-                t = psum.tile([P, 512], BF16, name="tp%d_%d_%d" % (r, c, bb), tag="bank")
-                for tt in range(4):
-                    nc.tensor.transpose(t[:, tt * P:(tt + 1) * P], xwb[(c, bb)][:, tt * P:(tt + 1) * P], ident_b[:])
-                tp[(c, bb)] = t
-            if r == NR - 1:
-                for G in range(NG - UNITS):
-                    for bb in range(NB):
-                        second_stage(G, bb)
-            xwg = {}
-            for c in range(UNITS):
-                xwg[c] = work.tile([P, 1024], BF16, name="xwg%d_%d" % (r, c), tag="xwg", align_bytes=64)
+                transpose_unit(r, c, bb)
             for i, (c, bb) in enumerate(units):
-                dst = xwg[c][:, bb * 512:(bb + 1) * 512].rearrange("p (i t) -> p i t", t=4)
-                src = tp[(c, bb)][:].rearrange("p (t i) -> p i t", t=4)
-                if i % 2 == 0:
-                    nc.scalar.copy(out=dst, in_=src)
-                else:
-                    nc.vector.tensor_copy(out=dst, in_=src)
-            for c in range(UNITS):
-                G = r * UNITS + c
-                xwc[G] = keep.tile([P, 256], U32, name="xwc%d" % G, align_bytes=64)
-                xws[G] = keep.tile([P, 256], U8, name="xws%d" % G, align_bytes=64)
-                nc.vector.quantize_mx(out=xwc[G][:].bitcast(FP8X4), scales=xws[G][:], in_=xwg[c][:])
+                regroup_unit(r, c, bb, i % 2 == 1)
+            for (c, bb) in units:
+                quantise_unit(r, c, bb)
 
-        for G in range(NG - UNITS, NG):
+        left = [(0, bb) for bb in range(NB)]
+        right = [(1, bb) for bb in range(NB)]
+        for (c, bb) in units:
+            acc[(LAST, c, bb)] = psum.tile([P, 512], F32, name="acc%d_%d_%d" % (LAST, c, bb), tag="bank")
+        for g in range(4):
+            first_stage(LAST, g, units)
+        for g in range(4, NG):
+            first_stage(LAST, g, left)
+        for (c, bb) in left:
+            leave_bank(LAST, c, bb, bb == 0)
+        for g in range(4, 6):
+            first_stage(LAST, g, right)
+        for bb in range(NB):
+            sc.append(psum.tile([P, 512], F32, name="sc%d" % bb, tag="bank"))
+        for (c, bb) in left:
+            transpose_unit(LAST, c, bb)
+        for g in range(6, NG):
+            first_stage(LAST, g, right)
+        for (c, bb) in left:
+            regroup_unit(LAST, c, bb, bb == 0)
+        for (c, bb) in left:
+            quantise_unit(LAST, c, bb)
+        for (c, bb) in right:
+            leave_bank(LAST, c, bb, bb == 0)
+        for (c, bb) in right:
+            transpose_unit(LAST, c, bb)
+        for G in range(NG - 1):
             for bb in range(NB):
                 second_stage(G, bb)
+        for (c, bb) in right:
+            regroup_unit(LAST, c, bb, bb == 0)
+        for (c, bb) in right:
+            quantise_unit(LAST, c, bb)
+
         res = keep.tile([P, NB * P], F32, name="res")
+        for bb in range(NB):
+            second_stage(NG - 1, bb)
         for bb in range(NB):
             nc.vector.scalar_tensor_tensor(
                 out=res[:, bb * P:(bb + 1) * P],

@@ -71,42 +71,32 @@ def tile_readingorderhead_w_kernel(tc, panel_embeddings, W_words, W_scales, b, o
                     in_=W_scales[4 * h:4 * h + 4, 4 * q:4 * q + 4, c0:c0 + ROUND_COLS].bitcast(I32),
                 )
 
-        def load_w(r, g, halves):
-            c0 = r * ROUND_COLS + halves[0] * 512
-            n = len(halves) * 512
-            wt = keep.tile([P, n], U32, name="w%d_%d_%d" % (r, g, halves[0]), align_bytes=256)
+        def load_w(r, g):
+            c0 = r * ROUND_COLS
+            wt = keep.tile([P, ROUND_COLS], U32, name="w%d_%d" % (r, g), align_bytes=256)
             nc.sync.dma_start(
                 out=wt[:].bitcast(I32),
-                in_=W_words[g].rearrange("p n t -> p (n t)")[:, 4 * c0:4 * (c0 + n)].bitcast(I32),
+                in_=W_words[g].rearrange("p n t -> p (n t)")[:, 4 * c0:4 * (c0 + ROUND_COLS)].bitcast(I32),
             )
-            for i, c in enumerate(halves):
-                w_sb[(r, g, c)] = wt[:, i * 512:(i + 1) * 512]
+            w_sb[(r, g)] = wt
 
-        LAST = NR - 1
         load_x(0)
         load_x(1)
         load_scales(0, 0)
-        load_w(0, 0, [0, 1])
-        load_w(0, 1, [0, 1])
+        load_w(0, 0)
+        load_w(0, 1)
         load_x(2)
-        load_w(0, 2, [0, 1])
-        load_w(0, 3, [0, 1])
+        load_w(0, 2)
+        load_w(0, 3)
         load_x(3)
         load_scales(0, 1)
         for g in range(4, NG):
-            load_w(0, g, [0, 1])
-        for r in range(1, LAST):
+            load_w(0, g)
+        for r in range(1, NR):
             for g in range(NG):
                 if g % 4 == 0:
                     load_scales(r, g // 4)
-                load_w(r, g, [0, 1])
-        load_scales(LAST, 0)
-        for g in range(4):
-            load_w(LAST, g, [0, 1])
-        load_scales(LAST, 1)
-        for c in range(UNITS):
-            for g in range(4, NG):
-                load_w(LAST, g, [c])
+                load_w(r, g)
 
         xc = {}
         xs = {}
@@ -147,78 +137,36 @@ def tile_readingorderhead_w_kernel(tc, panel_embeddings, W_words, W_scales, b, o
                 xs[g // 2][:, j * 256:j * 256 + P],
             )
 
-        acc = {}
-        xwb = {}
-        tp = {}
-        xwg = {}
         xwc = {}
         xws = {}
         sc = []
         units = [(c, bb) for c in range(UNITS) for bb in range(NB)]
 
-        def first_stage(r, g, which):
-            h, kk = g // 4, g % 4
-            for (c, bb) in which:
-                lhsT, lhsT_s = x_slice(g, bb)
-                nc.tensor.matmul_mx(
-                    out=acc[(r, c, bb)][:],
-                    lhsT=lhsT,
-                    lhsT_scale=lhsT_s,
-                    rhs=w_sb[(r, g, c)].bitcast(FP8X4),
-                    rhs_scale=planes[(r, h)][4 * kk:P, c * 512:(c + 1) * 512],
-                    start=(g == 0),
-                    stop=(g == NG - 1),
-                )
-
-        def copy_on(on_vector, dst, src):
-            if on_vector:
-                nc.vector.tensor_copy(out=dst, in_=src)
-            else:
-                nc.scalar.copy(out=dst, in_=src)
-
-        def leave_bank(r, c, bb, on_vector):
-            t = work.tile([P, 512], BF16, name="xwb%d_%d_%d" % (r, c, bb), tag="xwb", bufs=8)
-            copy_on(
-                on_vector,
-                t[:].rearrange("p (t m) -> p t m", t=4),
-                acc[(r, c, bb)][:].rearrange("p (m t) -> p t m", t=4),
-            )
-            xwb[(r, c, bb)] = t
-
-        def transpose_unit(r, c, bb):
-            t = psum.tile([P, 512], BF16, name="tp%d_%d_%d" % (r, c, bb), tag="bank")
-            for tt in range(4):
-                nc.tensor.transpose(t[:, tt * P:(tt + 1) * P], xwb[(r, c, bb)][:, tt * P:(tt + 1) * P], ident_b[:])
-            tp[(r, c, bb)] = t
-
-        def regroup_unit(r, c, bb, on_vector):
-            t = work.tile([P, 512], BF16, name="xwg%d_%d_%d" % (r, c, bb), tag="xwg", bufs=8, align_bytes=64)
-            copy_on(
-                on_vector,
-                t[:].rearrange("p (i t) -> p i t", t=4),
-                tp[(r, c, bb)][:].rearrange("p (t i) -> p i t", t=4),
-            )
-            xwg[(r, c, bb)] = t
-
-        def quantise_unit(r, c, bb):
-            G = r * UNITS + c
-            xwc[(G, bb)] = keep.tile([P, P], U32, name="xwc%d_%d" % (G, bb), align_bytes=64)
-            xws[(G, bb)] = keep.tile([P, P], U8, name="xws%d_%d" % (G, bb), align_bytes=64)
-            nc.vector.quantize_mx(
-                out=xwc[(G, bb)][:].bitcast(FP8X4), scales=xws[(G, bb)][:], in_=xwg[(r, c, bb)][:]
-            )
-
         def second_stage(G, bb):
             rhs, rhs_s = x_slice(G, bb)
             nc.tensor.matmul_mx(
                 out=sc[bb][:, 0:P],
-                lhsT=xwc[(G, bb)][:].bitcast(FP8X4),
-                lhsT_scale=xws[(G, bb)][:],
+                lhsT=xwc[G][:, bb * P:(bb + 1) * P].bitcast(FP8X4),
+                lhsT_scale=xws[G][:, bb * P:(bb + 1) * P],
                 rhs=rhs,
                 rhs_scale=rhs_s,
                 start=(G == 0),
                 stop=(G == NG - 1),
             )
+
+        def first_stage(r, g, acc):
+            h, kk = g // 4, g % 4
+            for (c, bb) in units:
+                lhsT, lhsT_s = x_slice(g, bb)
+                nc.tensor.matmul_mx(
+                    out=acc[(c, bb)][:],
+                    lhsT=lhsT,
+                    lhsT_scale=lhsT_s,
+                    rhs=w_sb[(r, g)][:, c * 512:(c + 1) * 512].bitcast(FP8X4),
+                    rhs_scale=planes[(r, h)][4 * kk:P, c * 512:(c + 1) * 512],
+                    start=(g == 0),
+                    stop=(g == NG - 1),
+                )
 
         prepare_x(0)
         keep_clock_up(2)
@@ -229,61 +177,66 @@ def tile_readingorderhead_w_kernel(tc, panel_embeddings, W_words, W_scales, b, o
         bias_f = keep.tile([P, 1], F32, name="bias_f")
         nc.vector.tensor_copy(out=bias_f[:], in_=bias_b[:])
 
-        for r in range(LAST):
+        def finish_round(r, acc):
+            if r == NR - 1:
+                for bb in range(NB):
+                    sc.append(psum.tile([P, 512], F32, name="sc%d" % bb, tag="bank"))
+            xwb = {}
+            for i, (c, bb) in enumerate(units):
+                t = work.tile([P, 512], BF16, name="xwb%d_%d_%d" % (r, c, bb), tag="xwb", bufs=8)
+                dst = t[:].rearrange("p (t m) -> p t m", t=4)
+                src = acc[(c, bb)][:].rearrange("p (m t) -> p t m", t=4)
+                if i % 2 == 0:
+                    nc.scalar.copy(out=dst, in_=src)
+                else:
+                    nc.vector.tensor_copy(out=dst, in_=src)
+                xwb[(c, bb)] = t
+            tp = {}
             for (c, bb) in units:
-                acc[(r, c, bb)] = psum.tile([P, 512], F32, name="acc%d_%d_%d" % (r, c, bb), tag="bank")
+                t = psum.tile([P, 512], BF16, name="tp%d_%d_%d" % (r, c, bb), tag="bank")
+                for tt in range(4):
+                    nc.tensor.transpose(t[:, tt * P:(tt + 1) * P], xwb[(c, bb)][:, tt * P:(tt + 1) * P], ident_b[:])
+                tp[(c, bb)] = t
+            if r == NR - 1:
+                for G in range(NG - UNITS):
+                    for bb in range(NB):
+                        second_stage(G, bb)
+            xwg = {}
+            for c in range(UNITS):
+                xwg[c] = work.tile([P, 1024], BF16, name="xwg%d_%d" % (r, c), tag="xwg", align_bytes=64)
+            for i, (c, bb) in enumerate(units):
+                dst = xwg[c][:, bb * 512:(bb + 1) * 512].rearrange("p (i t) -> p i t", t=4)
+                src = tp[(c, bb)][:].rearrange("p (t i) -> p i t", t=4)
+                if i % 2 == 0:
+                    nc.scalar.copy(out=dst, in_=src)
+                else:
+                    nc.vector.tensor_copy(out=dst, in_=src)
+            for c in range(UNITS):
+                G = r * UNITS + c
+                xwc[G] = keep.tile([P, 256], U32, name="xwc%d" % G, align_bytes=64)
+                xws[G] = keep.tile([P, 256], U8, name="xws%d" % G, align_bytes=64)
+                nc.vector.quantize_mx(out=xwc[G][:].bitcast(FP8X4), scales=xws[G][:], in_=xwg[c][:])
+
+
+        accs = {}
+        for r in range(NR):
+            accs[r] = {}
+            for (c, bb) in units:
+                accs[r][(c, bb)] = psum.tile([P, 512], F32, name="acc%d_%d_%d" % (r, c, bb), tag="bank")
             for g in range(NG):
-                first_stage(r, g, units)
+                first_stage(r, g, accs[r])
+                if g == 0 and r > 0:
+                    finish_round(r - 1, accs[r - 1])
                 if r == 0 and g == 1:
                     prepare_x(2)
                 if r == 0 and g == 3:
                     prepare_x(3)
-            for i, (c, bb) in enumerate(units):
-                leave_bank(r, c, bb, i % 2 == 1)
-            for (c, bb) in units:
-                transpose_unit(r, c, bb)
-            for i, (c, bb) in enumerate(units):
-                regroup_unit(r, c, bb, i % 2 == 1)
-            for (c, bb) in units:
-                quantise_unit(r, c, bb)
+        finish_round(NR - 1, accs[NR - 1])
 
-        left = [(0, bb) for bb in range(NB)]
-        right = [(1, bb) for bb in range(NB)]
-        for (c, bb) in units:
-            acc[(LAST, c, bb)] = psum.tile([P, 512], F32, name="acc%d_%d_%d" % (LAST, c, bb), tag="bank")
-        for g in range(4):
-            first_stage(LAST, g, units)
-        for g in range(4, NG):
-            first_stage(LAST, g, left)
-        for (c, bb) in left:
-            leave_bank(LAST, c, bb, bb == 0)
-        for g in range(4, 6):
-            first_stage(LAST, g, right)
-        for bb in range(NB):
-            sc.append(psum.tile([P, 512], F32, name="sc%d" % bb, tag="bank"))
-        for (c, bb) in left:
-            transpose_unit(LAST, c, bb)
-        for g in range(6, NG):
-            first_stage(LAST, g, right)
-        for (c, bb) in left:
-            regroup_unit(LAST, c, bb, bb == 0)
-        for (c, bb) in left:
-            quantise_unit(LAST, c, bb)
-        for (c, bb) in right:
-            leave_bank(LAST, c, bb, bb == 0)
-        for (c, bb) in right:
-            transpose_unit(LAST, c, bb)
-        for G in range(NG - 1):
+        for G in range(NG - UNITS, NG):
             for bb in range(NB):
                 second_stage(G, bb)
-        for (c, bb) in right:
-            regroup_unit(LAST, c, bb, bb == 0)
-        for (c, bb) in right:
-            quantise_unit(LAST, c, bb)
-
         res = keep.tile([P, NB * P], F32, name="res")
-        for bb in range(NB):
-            second_stage(NG - 1, bb)
         for bb in range(NB):
             nc.vector.scalar_tensor_tensor(
                 out=res[:, bb * P:(bb + 1) * P],

@@ -51,15 +51,18 @@ def tile_readingorderhead_w_kernel(tc, panel_embeddings, W_words, W_scales, b, o
         make_identity(nc, ident_f[:])
         ident_b = keep.tile([P, P], BF16, name="ident_b")
         make_identity(nc, ident_b[:])
-        bias_b = keep.tile([P, 1], BF16, name="bias_b")
-        nc.scalar.dma_start(out=bias_b[:], in_=b.partition_broadcast(P))
+        bias_row = keep.tile([P, 32], BF16, name="bias_row")
+        nc.vector.memset(bias_row[:], 0.0)
+        nc.scalar.dma_start(out=bias_row[0:1, 0:1], in_=b.rearrange("(o n) -> o n", o=1))
+        ones = keep.tile([P, P], BF16, name="ones")
+        nc.vector.memset(ones[:], 1.0)
 
         xv = panel_embeddings.rearrange("b i d -> i b d")
         x_sb = {}
         w_sb = {}
 
         def load_x(qq):
-            t = keep.tile([P, NB, 1024], BF16, name="x_sb%d" % qq)
+            t = keep.tile([P, NB, 1024], BF16, name="x_sb%d" % qq, align_bytes=256)
             nc.sync.dma_start(out=t[:], in_=xv[:, :, qq * 1024:(qq + 1) * 1024])
             x_sb[qq] = t
 
@@ -174,10 +177,20 @@ def tile_readingorderhead_w_kernel(tc, panel_embeddings, W_words, W_scales, b, o
         keep_clock_up(2)
         mask = keep.tile([P, P], F32, name="mask")
         nc.vector.tensor_scalar(out=mask[:], in0=ident_f[:], scalar1=-1.0, scalar2=1.0, op0=ALU.mult, op1=ALU.add)
+        nc.tensor.matmul(out=warm[:, 0:32], lhsT=ones[:], rhs=bias_row[:], start=True, stop=True)
         bias_f = keep.tile([P, 1], F32, name="bias_f")
-        nc.vector.tensor_copy(out=bias_f[:], in_=bias_b[:])
+        nc.vector.tensor_copy(out=bias_f[:], in_=warm[:, 0:1])
 
-        def finish_round(r, acc):
+        for r in range(NR):
+            acc = {}
+            for (c, bb) in units:
+                acc[(c, bb)] = psum.tile([P, 512], F32, name="acc%d_%d_%d" % (r, c, bb), tag="bank")
+            for g in range(NG):
+                first_stage(r, g, acc)
+                if r == 0 and g == 1:
+                    prepare_x(2)
+                if r == 0 and g == 3:
+                    prepare_x(3)
             if r == NR - 1:
                 for bb in range(NB):
                     sc.append(psum.tile([P, 512], F32, name="sc%d" % bb, tag="bank"))
@@ -217,26 +230,10 @@ def tile_readingorderhead_w_kernel(tc, panel_embeddings, W_words, W_scales, b, o
                 xws[G] = keep.tile([P, 256], U8, name="xws%d" % G, align_bytes=64)
                 nc.vector.quantize_mx(out=xwc[G][:].bitcast(FP8X4), scales=xws[G][:], in_=xwg[c][:])
 
-
-        accs = {}
-        for r in range(NR):
-            accs[r] = {}
-            for (c, bb) in units:
-                accs[r][(c, bb)] = psum.tile([P, 512], F32, name="acc%d_%d_%d" % (r, c, bb), tag="bank")
-            for g in range(NG):
-                first_stage(r, g, accs[r])
-                if g == 0 and r > 0:
-                    finish_round(r - 1, accs[r - 1])
-                if r == 0 and g == 1:
-                    prepare_x(2)
-                if r == 0 and g == 3:
-                    prepare_x(3)
-        finish_round(NR - 1, accs[NR - 1])
-
         for G in range(NG - UNITS, NG):
             for bb in range(NB):
                 second_stage(G, bb)
-        res = keep.tile([P, NB * P], F32, name="res")
+        res = keep.tile([P, NB * P], F32, name="res", align_bytes=256)
         for bb in range(NB):
             nc.vector.scalar_tensor_tensor(
                 out=res[:, bb * P:(bb + 1) * P],

@@ -12,235 +12,222 @@ FP8X4 = mybir.dt.float8_e4m3fn_x4
 ALU = mybir.AluOpType
 
 P = 128
-NB = 2
+BATCHES = 2
 D = 4096
-K_PASS = 512
-NG = D // K_PASS
-ROUND_COLS = 1024
-NR = D // ROUND_COLS
-UNITS = ROUND_COLS // K_PASS
-PAD_WORDS = 48
+PACK = 4
+GROUP = P * PACK
+GROUPS = D // GROUP
+ROUND = 2 * GROUP
+ROUNDS = D // ROUND
+HALVES = ROUND // GROUP
+QUADRANT = 32
+PLANE_ROWS = QUADRANT // 8
+SHARED = 4
+LINE = 256
+X_WORDS_PAD = 192 // 4
 
-FLOPS = 2 * NB * P * D * D + 2 * NB * P * P * D
+FLOPS = 2 * BATCHES * P * D * D + 2 * BATCHES * P * P * D
 
 
 def tile_readingorderhead_w_kernel(tc, panel_embeddings, W_words, W_scales, b, out):
     nc = tc.nc
+    units = [(half, batch) for half in range(HALVES) for batch in range(BATCHES)]
+
     with ExitStack() as ctx:
         keep = ctx.enter_context(tc.tile_pool(name="keep", bufs=1))
         work = ctx.enter_context(tc.tile_pool(name="work", bufs=4))
         psum = ctx.enter_context(tc.psum_pool(name="psum", bufs=8))
         ctx.enter_context(tc.manual_schedule())
 
-        zeros = keep.tile([P, 512], BF16, name="zeros")
-        nc.vector.memset(zeros[:], 0.0)
-        warm = psum.tile([P, 512], F32, name="warm", tag="bank")
+        def copy_on(on_vector, dst, src):
+            if on_vector:
+                nc.vector.tensor_copy(out=dst, in_=src)
+            else:
+                nc.scalar.copy(out=dst, in_=src)
 
-        def keep_clock_up(n):
-            for rep in range(n):
-                nc.tensor.matmul(out=warm[:], lhsT=zeros[:, 0:P], rhs=zeros[:], start=True, stop=True)
+        w_planes = {}
+        for r in range(ROUNDS):
+            for s in range(GROUPS // SHARED):
+                w_planes[(r, s)] = keep.tile([P, ROUND], U8, name="w_planes%d_%d" % (r, s), align_bytes=LINE)
+                nc.vector.memset(w_planes[(r, s)][:].bitcast(I32), 0)
+        ident_f32 = keep.tile([P, P], F32, name="ident_f32")
+        make_identity(nc, ident_f32[:])
+        ident_bf16 = keep.tile([P, P], BF16, name="ident_bf16")
+        make_identity(nc, ident_bf16[:])
+        bias_bf16 = keep.tile([P, 1], BF16, name="bias_bf16")
+        nc.scalar.dma_start(out=bias_bf16[:], in_=b.partition_broadcast(P))
 
-        keep_clock_up(6)
-        planes = {}
-        for r in range(NR):
-            for h in range(2):
-                pl = keep.tile([P, ROUND_COLS], U8, name="wpl%d_%d" % (r, h), align_bytes=256)
-                nc.vector.memset(pl[:].bitcast(I32), 0)
-                planes[(r, h)] = pl
-        ident_f = keep.tile([P, P], F32, name="ident_f")
-        make_identity(nc, ident_f[:])
-        ident_b = keep.tile([P, P], BF16, name="ident_b")
-        make_identity(nc, ident_b[:])
-        bias_row = keep.tile([P, 32], BF16, name="bias_row")
-        nc.vector.memset(bias_row[:], 0.0)
-        nc.scalar.dma_start(out=bias_row[0:1, 0:1], in_=b.rearrange("(o n) -> o n", o=1))
-        ones = keep.tile([P, P], BF16, name="ones")
-        nc.vector.memset(ones[:], 1.0)
+        x_rows = panel_embeddings.rearrange("b i d -> i b d")
+        x_sb = []
+        for side in range(2):
+            x_sb.append(keep.tile([P, BATCHES, D // 2], BF16, name="x_sb%d" % side, align_bytes=LINE))
+            nc.sync.dma_start(out=x_sb[side][:], in_=x_rows[:, :, side * (D // 2):(side + 1) * (D // 2)])
+        w_words = {}
 
-        xv = panel_embeddings.rearrange("b i d -> i b d")
-        x_sb = {}
-        w_sb = {}
-
-        def load_x(qq):
-            t = keep.tile([P, NB, 1024], BF16, name="x_sb%d" % qq, align_bytes=256)
-            nc.sync.dma_start(out=t[:], in_=xv[:, :, qq * 1024:(qq + 1) * 1024])
-            x_sb[qq] = t
-
-        def load_scales(r, h):
-            c0 = r * ROUND_COLS
-            for q in range(4):
+        def load_w(r, g, pieces):
+            width = ROUND // pieces
+            for piece in range(pieces):
+                lo = r * ROUND + piece * width
+                chunk = keep.tile([P, width], U32, name="w_words%d_%d_%d" % (r, g, piece), align_bytes=LINE)
                 nc.sync.dma_start(
-                    out=planes[(r, h)][32 * q:32 * q + 16, :].bitcast(I32),
-                    in_=W_scales[4 * h:4 * h + 4, 4 * q:4 * q + 4, c0:c0 + ROUND_COLS].bitcast(I32),
+                    out=chunk[:].bitcast(I32),
+                    in_=W_words[g].rearrange("p n t -> p (n t)")[:, PACK * lo:PACK * (lo + width)].bitcast(I32),
                 )
+                for k in range(width // GROUP):
+                    w_words[(r, g, piece * width // GROUP + k)] = chunk[:, k * GROUP:(k + 1) * GROUP]
 
-        def load_w(r, g):
-            c0 = r * ROUND_COLS
-            wt = keep.tile([P, ROUND_COLS], U32, name="w%d_%d" % (r, g), align_bytes=256)
-            nc.sync.dma_start(
-                out=wt[:].bitcast(I32),
-                in_=W_words[g].rearrange("p n t -> p (n t)")[:, 4 * c0:4 * (c0 + ROUND_COLS)].bitcast(I32),
-            )
-            w_sb[(r, g)] = wt
-
-        load_x(0)
-        load_x(1)
-        load_scales(0, 0)
-        load_w(0, 0)
-        load_w(0, 1)
-        load_x(2)
-        load_w(0, 2)
-        load_w(0, 3)
-        load_x(3)
-        load_scales(0, 1)
-        for g in range(4, NG):
-            load_w(0, g)
-        for r in range(1, NR):
-            for g in range(NG):
-                if g % 4 == 0:
-                    load_scales(r, g // 4)
-                load_w(r, g)
-
-        xc = {}
-        xs = {}
-
-        def prepare_x(qq):
-            xg = work.tile([P, 2048], BF16, name="xg%d" % qq, tag="xg", align_bytes=64)
-            xc[qq] = keep.tile([P, PAD_WORDS + 512], U32, name="xc%d" % qq, align_bytes=256)
-            xs[qq] = keep.tile([P, 4 * 256], U8, name="xs%d" % qq, align_bytes=256)
-            for gl in range(2):
-                xt = psum.tile([P, 512], F32, name="xt%d_%d" % (qq, gl), tag="bank")
-                for bb in range(NB):
-                    words = x_sb[qq][:, bb, :].bitcast(F32)
-                    for u in range(2):
-                        nc.tensor.transpose(
-                            xt[:, (bb * 2 + u) * P:(bb * 2 + u + 1) * P],
-                            words[:, 256 * gl + u:256 * (gl + 1):2],
-                            ident_f[:],
+        for r in range(ROUNDS):
+            for g in range(GROUPS):
+                if g % SHARED == 0:
+                    s = g // SHARED
+                    for quadrant in range(P // QUADRANT):
+                        nc.sync.dma_start(
+                            out=w_planes[(r, s)][
+                                QUADRANT * quadrant:QUADRANT * quadrant + SHARED * PLANE_ROWS, :
+                            ].bitcast(I32),
+                            in_=W_scales[
+                                g:g + SHARED,
+                                PLANE_ROWS * quadrant:PLANE_ROWS * (quadrant + 1),
+                                r * ROUND:(r + 1) * ROUND,
+                            ].bitcast(I32),
                         )
-                dst = xg[:].bitcast(F32)[:, gl * 512:(gl + 1) * 512]
-                dst = dst.rearrange("p (b i u) -> p b i u", b=NB, u=2)
-                src = xt[:].rearrange("p (b u i) -> p b i u", b=NB, u=2)
-                if gl == 0:
-                    nc.vector.tensor_copy(out=dst, in_=src)
-                else:
-                    nc.scalar.copy(out=dst, in_=src)
-                for bb in range(NB):
-                    j = gl * NB + bb
-                    nc.vector.quantize_mx(
-                        out=xc[qq][:, PAD_WORDS + j * P:PAD_WORDS + (j + 1) * P].bitcast(FP8X4),
-                        scales=xs[qq][:, j * 256:j * 256 + P],
-                        in_=xg[:, j * 512:(j + 1) * 512],
-                    )
+                load_w(r, g, HALVES if (r, g) == (ROUNDS - 1, GROUPS - 1) else 1)
 
-        def x_slice(g, bb):
-            j = (g % 2) * NB + bb
-            return (
-                xc[g // 2][:, PAD_WORDS + j * P:PAD_WORDS + (j + 1) * P].bitcast(FP8X4),
-                xs[g // 2][:, j * 256:j * 256 + P],
-            )
+        x_codes = {}
+        x_scales = {}
+        x_grouped = {}
 
-        xwc = {}
-        xws = {}
-        sc = []
-        units = [(c, bb) for c in range(UNITS) for bb in range(NB)]
-
-        def second_stage(G, bb):
-            rhs, rhs_s = x_slice(G, bb)
-            nc.tensor.matmul_mx(
-                out=sc[bb][:, 0:P],
-                lhsT=xwc[G][:, bb * P:(bb + 1) * P].bitcast(FP8X4),
-                lhsT_scale=xws[G][:, bb * P:(bb + 1) * P],
-                rhs=rhs,
-                rhs_scale=rhs_s,
-                start=(G == 0),
-                stop=(G == NG - 1),
-            )
-
-        def first_stage(r, g, acc):
-            h, kk = g // 4, g % 4
-            for (c, bb) in units:
-                lhsT, lhsT_s = x_slice(g, bb)
-                nc.tensor.matmul_mx(
-                    out=acc[(c, bb)][:],
-                    lhsT=lhsT,
-                    lhsT_scale=lhsT_s,
-                    rhs=w_sb[(r, g)][:, c * 512:(c + 1) * 512].bitcast(FP8X4),
-                    rhs_scale=planes[(r, h)][4 * kk:P, c * 512:(c + 1) * 512],
-                    start=(g == 0),
-                    stop=(g == NG - 1),
+        def quantise_x(g):
+            x_codes[g] = keep.tile([P, X_WORDS_PAD + BATCHES * P], U32, name="x_codes%d" % g, align_bytes=LINE)
+            x_scales[g] = keep.tile([P, BATCHES * LINE], U8, name="x_scales%d" % g, align_bytes=LINE)
+            for batch in range(BATCHES):
+                codes, scales = x_operand(g, batch)
+                nc.vector.quantize_mx(
+                    out=codes, scales=scales, in_=x_grouped[g][:, batch * GROUP:(batch + 1) * GROUP]
                 )
 
-        prepare_x(0)
-        keep_clock_up(2)
-        prepare_x(1)
-        keep_clock_up(2)
-        mask = keep.tile([P, P], F32, name="mask")
-        nc.vector.tensor_scalar(out=mask[:], in0=ident_f[:], scalar1=-1.0, scalar2=1.0, op0=ALU.mult, op1=ALU.add)
-        nc.tensor.matmul(out=warm[:, 0:32], lhsT=ones[:], rhs=bias_row[:], start=True, stop=True)
-        bias_f = keep.tile([P, 1], F32, name="bias_f")
-        nc.vector.tensor_copy(out=bias_f[:], in_=warm[:, 0:1])
+        def x_operand(g, batch):
+            lo = X_WORDS_PAD + batch * P
+            return x_codes[g][:, lo:lo + P].bitcast(FP8X4), x_scales[g][:, batch * LINE:batch * LINE + P]
 
-        for r in range(NR):
-            acc = {}
-            for (c, bb) in units:
-                acc[(c, bb)] = psum.tile([P, 512], F32, name="acc%d_%d_%d" % (r, c, bb), tag="bank")
-            for g in range(NG):
-                first_stage(r, g, acc)
-                if r == 0 and g == 1:
-                    prepare_x(2)
-                if r == 0 and g == 3:
-                    prepare_x(3)
-            if r == NR - 1:
-                for bb in range(NB):
-                    sc.append(psum.tile([P, 512], F32, name="sc%d" % bb, tag="bank"))
-            xwb = {}
-            for i, (c, bb) in enumerate(units):
-                t = work.tile([P, 512], BF16, name="xwb%d_%d_%d" % (r, c, bb), tag="xwb", bufs=8)
-                dst = t[:].rearrange("p (t m) -> p t m", t=4)
-                src = acc[(c, bb)][:].rearrange("p (m t) -> p t m", t=4)
-                if i % 2 == 0:
-                    nc.scalar.copy(out=dst, in_=src)
-                else:
-                    nc.vector.tensor_copy(out=dst, in_=src)
-                xwb[(c, bb)] = t
-            tp = {}
-            for (c, bb) in units:
-                t = psum.tile([P, 512], BF16, name="tp%d_%d_%d" % (r, c, bb), tag="bank")
-                for tt in range(4):
-                    nc.tensor.transpose(t[:, tt * P:(tt + 1) * P], xwb[(c, bb)][:, tt * P:(tt + 1) * P], ident_b[:])
-                tp[(c, bb)] = t
-            if r == NR - 1:
-                for G in range(NG - UNITS):
-                    for bb in range(NB):
-                        second_stage(G, bb)
-            xwg = {}
-            for c in range(UNITS):
-                xwg[c] = work.tile([P, 1024], BF16, name="xwg%d_%d" % (r, c), tag="xwg", align_bytes=64)
-            for i, (c, bb) in enumerate(units):
-                dst = xwg[c][:, bb * 512:(bb + 1) * 512].rearrange("p (i t) -> p i t", t=4)
-                src = tp[(c, bb)][:].rearrange("p (t i) -> p i t", t=4)
-                if i % 2 == 0:
-                    nc.scalar.copy(out=dst, in_=src)
-                else:
-                    nc.vector.tensor_copy(out=dst, in_=src)
-            for c in range(UNITS):
-                G = r * UNITS + c
-                xwc[G] = keep.tile([P, 256], U32, name="xwc%d" % G, align_bytes=64)
-                xws[G] = keep.tile([P, 256], U8, name="xws%d" % G, align_bytes=64)
-                nc.vector.quantize_mx(out=xwc[G][:].bitcast(FP8X4), scales=xws[G][:], in_=xwg[c][:])
+        for g in range(GROUPS):
+            side, local = g // (GROUPS // 2), g % (GROUPS // 2)
+            bank = psum.tile([P, GROUP], F32, name="x_t%d" % g, tag="bank")
+            for batch in range(BATCHES):
+                words = x_sb[side][:, batch, :].bitcast(F32)
+                for u in range(2):
+                    nc.tensor.transpose(
+                        bank[:, (2 * batch + u) * P:(2 * batch + u + 1) * P],
+                        words[:, 2 * P * local + u:2 * P * (local + 1):2],
+                        ident_f32[:],
+                    )
+            x_grouped[g] = work.tile([P, BATCHES * GROUP], BF16, name="x_grouped%d" % g, tag="x_grouped", align_bytes=64)
+            copy_on(
+                g % 2 == 0,
+                x_grouped[g][:].bitcast(F32).rearrange("p (b i u) -> p b i u", b=BATCHES, u=2),
+                bank[:].rearrange("p (b u i) -> p b i u", b=BATCHES, u=2),
+            )
+            if g > 0:
+                quantise_x(g - 1)
+        quantise_x(GROUPS - 1)
 
-        for G in range(NG - UNITS, NG):
-            for bb in range(NB):
-                second_stage(G, bb)
-        res = keep.tile([P, NB * P], F32, name="res", align_bytes=256)
-        for bb in range(NB):
+        off_diagonal = keep.tile([P, P], F32, name="off_diagonal")
+        nc.vector.tensor_scalar(
+            out=off_diagonal[:], in0=ident_f32[:], scalar1=-1.0, scalar2=1.0, op0=ALU.mult, op1=ALU.add
+        )
+        bias_f32 = keep.tile([P, 1], F32, name="bias_f32")
+        nc.vector.tensor_copy(out=bias_f32[:], in_=bias_bf16[:])
+
+        xw_codes = {}
+        xw_scales = {}
+        scores = []
+
+        def second_matmul(group, batch):
+            rhs, rhs_scale = x_operand(group, batch)
+            nc.tensor.matmul_mx(
+                out=scores[batch][:, 0:P],
+                lhsT=xw_codes[group][:, batch * P:(batch + 1) * P].bitcast(FP8X4),
+                lhsT_scale=xw_scales[group][:, batch * P:(batch + 1) * P],
+                rhs=rhs,
+                rhs_scale=rhs_scale,
+                start=(group == 0),
+                stop=(group == GROUPS - 1),
+            )
+
+        for r in range(ROUNDS):
+            last = r == ROUNDS - 1
+            sums = {}
+            for unit in units:
+                sums[unit] = psum.tile([P, GROUP], F32, name="sums%d_%d_%d" % ((r,) + unit), tag="bank")
+            for g in range(GROUPS):
+                for (half, batch) in units:
+                    lhsT, lhsT_scale = x_operand(g, batch)
+                    nc.tensor.matmul_mx(
+                        out=sums[(half, batch)][:],
+                        lhsT=lhsT,
+                        lhsT_scale=lhsT_scale,
+                        rhs=w_words[(r, g, half)].bitcast(FP8X4),
+                        rhs_scale=w_planes[(r, g // SHARED)][
+                            PLANE_ROWS * (g % SHARED):P, half * GROUP:(half + 1) * GROUP
+                        ],
+                        start=(g == 0),
+                        stop=(g == GROUPS - 1),
+                    )
+            if last:
+                for batch in range(BATCHES):
+                    scores.append(psum.tile([P, GROUP], F32, name="scores%d" % batch, tag="bank"))
+
+            xw_bf16 = {}
+            for i, unit in enumerate(units):
+                xw_bf16[unit] = work.tile([P, GROUP], BF16, name="xw_bf16_%d_%d_%d" % ((r,) + unit), tag="xw_bf16", bufs=8)
+                copy_on(
+                    i % 2 == 1,
+                    xw_bf16[unit][:].rearrange("p (t m) -> p t m", t=PACK),
+                    sums[unit][:].rearrange("p (m t) -> p t m", t=PACK),
+                )
+            xw_t = {}
+            for unit in units:
+                xw_t[unit] = psum.tile([P, GROUP], BF16, name="xw_t%d_%d_%d" % ((r,) + unit), tag="bank")
+                for t in range(PACK):
+                    nc.tensor.transpose(
+                        xw_t[unit][:, t * P:(t + 1) * P], xw_bf16[unit][:, t * P:(t + 1) * P], ident_bf16[:]
+                    )
+            if last:
+                for group in range(GROUPS - HALVES):
+                    for batch in range(BATCHES):
+                        second_matmul(group, batch)
+            xw_grouped = {}
+            for i, (half, batch) in enumerate(units):
+                if batch == 0:
+                    xw_grouped[half] = work.tile(
+                        [P, BATCHES * GROUP], BF16, name="xw_grouped%d_%d" % (r, half), tag="xw_grouped", align_bytes=64
+                    )
+                copy_on(
+                    i % 2 == 1,
+                    xw_grouped[half][:, batch * GROUP:(batch + 1) * GROUP].rearrange("p (i t) -> p i t", t=PACK),
+                    xw_t[(half, batch)][:].rearrange("p (t i) -> p i t", t=PACK),
+                )
+            for half in range(HALVES):
+                group = r * HALVES + half
+                xw_codes[group] = keep.tile([P, BATCHES * P], U32, name="xw_codes%d" % group, align_bytes=64)
+                xw_scales[group] = keep.tile([P, BATCHES * P], U8, name="xw_scales%d" % group, align_bytes=64)
+                nc.vector.quantize_mx(
+                    out=xw_codes[group][:].bitcast(FP8X4), scales=xw_scales[group][:], in_=xw_grouped[half][:]
+                )
+
+        for group in range(GROUPS - HALVES, GROUPS):
+            for batch in range(BATCHES):
+                second_matmul(group, batch)
+        result = keep.tile([P, BATCHES * P], F32, name="result")
+        for batch in range(BATCHES):
             nc.vector.scalar_tensor_tensor(
-                out=res[:, bb * P:(bb + 1) * P],
-                in0=sc[bb][:, 0:P],
-                scalar=bias_f[:, 0:1],
-                in1=mask[:],
+                out=result[:, batch * P:(batch + 1) * P],
+                in0=scores[batch][:, 0:P],
+                scalar=bias_f32[:, 0:1],
+                in1=off_diagonal[:],
                 op0=ALU.add,
                 op1=ALU.mult,
             )
-        nc.sync.dma_start(out=out.rearrange("b i j -> i b j"), in_=res[:].rearrange("p (b j) -> p b j", b=NB))
+        nc.sync.dma_start(
+            out=out.rearrange("b i j -> i b j"), in_=result[:].rearrange("p (b j) -> p b j", b=BATCHES)
+        )

@@ -17,27 +17,34 @@ D = 4096
 PACK = 4
 GROUP = P * PACK
 GROUPS = D // GROUP
-ROUND = 2 * GROUP
-ROUNDS = D // ROUND
-HALVES = ROUND // GROUP
+RANGE = 2 * GROUP
+RANGES = D // RANGE
+ROUND_GROUPS = [2,2,2,1,1]
+LEAD = 1
 QUADRANT = 32
 PLANE_ROWS = QUADRANT // 8
 SHARED = 4
 LINE = 256
 X_WORDS_PAD = 192 // 4
+X_PIECES = 4
+EARLY_FIRST = 4
 
 FLOPS = 2 * BATCHES * P * D * D + 2 * BATCHES * P * P * D
 
 
 def tile_readingorderhead_w_kernel(tc, panel_embeddings, W_words, W_scales, b, out):
     nc = tc.nc
-    units = [(half, batch) for half in range(HALVES) for batch in range(BATCHES)]
+    rounds = len(ROUND_GROUPS)
+    first_group = [sum(ROUND_GROUPS[:r]) for r in range(rounds)]
 
     with ExitStack() as ctx:
         keep = ctx.enter_context(tc.tile_pool(name="keep", bufs=1))
         work = ctx.enter_context(tc.tile_pool(name="work", bufs=4))
-        psum = ctx.enter_context(tc.psum_pool(name="psum", bufs=8))
+        psum = ctx.enter_context(tc.psum_pool(name="psum", bufs=1))
         ctx.enter_context(tc.manual_schedule())
+
+        def bank(k, dtype, name):
+            return psum.tile([P, GROUP], dtype, name=name, tag="bank%d" % k)
 
         def copy_on(on_vector, dst, src):
             if on_vector:
@@ -46,56 +53,62 @@ def tile_readingorderhead_w_kernel(tc, panel_embeddings, W_words, W_scales, b, o
                 nc.scalar.copy(out=dst, in_=src)
 
         w_planes = {}
-        for r in range(ROUNDS):
+        for c in range(RANGES):
             for s in range(GROUPS // SHARED):
-                w_planes[(r, s)] = keep.tile([P, ROUND], U8, name="w_planes%d_%d" % (r, s), align_bytes=LINE)
-                nc.vector.memset(w_planes[(r, s)][:].bitcast(I32), 0)
+                w_planes[(c, s)] = keep.tile([P, RANGE], U8, name="w_planes%d_%d" % (c, s), align_bytes=LINE)
+                nc.vector.memset(w_planes[(c, s)][:].bitcast(I32), 0)
         ident_f32 = keep.tile([P, P], F32, name="ident_f32")
         make_identity(nc, ident_f32[:])
-        ident_bf16 = keep.tile([P, P], BF16, name="ident_bf16")
-        make_identity(nc, ident_bf16[:])
         bias_bf16 = keep.tile([P, 1], BF16, name="bias_bf16")
         nc.scalar.dma_start(out=bias_bf16[:], in_=b.partition_broadcast(P))
 
         x_rows = panel_embeddings.rearrange("b i d -> i b d")
         x_sb = []
-        for side in range(2):
-            x_sb.append(keep.tile([P, BATCHES, D // 2], BF16, name="x_sb%d" % side, align_bytes=LINE))
-            nc.sync.dma_start(out=x_sb[side][:], in_=x_rows[:, :, side * (D // 2):(side + 1) * (D // 2)])
+        for piece in range(X_PIECES):
+            x_sb.append(keep.tile([P, BATCHES, D // X_PIECES], BF16, name="x_sb%d" % piece, align_bytes=LINE))
+            nc.sync.dma_start(
+                out=x_sb[piece][:], in_=x_rows[:, :, piece * (D // X_PIECES):(piece + 1) * (D // X_PIECES)]
+            )
         w_words = {}
 
-        def load_w(r, g, pieces):
-            width = ROUND // pieces
-            for piece in range(pieces):
-                lo = r * ROUND + piece * width
-                chunk = keep.tile([P, width], U32, name="w_words%d_%d_%d" % (r, g, piece), align_bytes=LINE)
+        def load_planes(c, s):
+            for quadrant in range(P // QUADRANT):
                 nc.sync.dma_start(
-                    out=chunk[:].bitcast(I32),
-                    in_=W_words[g].rearrange("p n t -> p (n t)")[:, PACK * lo:PACK * (lo + width)].bitcast(I32),
+                    out=w_planes[(c, s)][QUADRANT * quadrant:QUADRANT * quadrant + SHARED * PLANE_ROWS, :].bitcast(I32),
+                    in_=W_scales[
+                        s * SHARED:(s + 1) * SHARED,
+                        PLANE_ROWS * quadrant:PLANE_ROWS * (quadrant + 1),
+                        c * RANGE:(c + 1) * RANGE,
+                    ].bitcast(I32),
                 )
-                for k in range(width // GROUP):
-                    w_words[(r, g, piece * width // GROUP + k)] = chunk[:, k * GROUP:(k + 1) * GROUP]
 
-        for r in range(ROUNDS):
+        def load_w(r, g):
+            lo = first_group[r] * GROUP
+            width = ROUND_GROUPS[r] * GROUP
+            chunk = keep.tile([P, width], U32, name="w_words%d_%d" % (r, g), align_bytes=LINE)
+            nc.sync.dma_start(
+                out=chunk[:].bitcast(I32),
+                in_=W_words[g].rearrange("p n t -> p (n t)")[:, PACK * lo:PACK * (lo + width)].bitcast(I32),
+            )
+            for half in range(ROUND_GROUPS[r]):
+                w_words[(r, g, half)] = chunk[:, half * GROUP:(half + 1) * GROUP]
+
+        planes_loaded = set()
+        for r in range(rounds):
+            c = first_group[r] * GROUP // RANGE
             for g in range(GROUPS):
-                if g % SHARED == 0:
-                    s = g // SHARED
-                    for quadrant in range(P // QUADRANT):
-                        nc.sync.dma_start(
-                            out=w_planes[(r, s)][
-                                QUADRANT * quadrant:QUADRANT * quadrant + SHARED * PLANE_ROWS, :
-                            ].bitcast(I32),
-                            in_=W_scales[
-                                g:g + SHARED,
-                                PLANE_ROWS * quadrant:PLANE_ROWS * (quadrant + 1),
-                                r * ROUND:(r + 1) * ROUND,
-                            ].bitcast(I32),
-                        )
-                load_w(r, g, HALVES if (r, g) == (ROUNDS - 1, GROUPS - 1) else 1)
+                if g % SHARED == 0 and (c, g // SHARED) not in planes_loaded:
+                    planes_loaded.add((c, g // SHARED))
+                    load_planes(c, g // SHARED)
+                load_w(r, g)
 
         x_codes = {}
         x_scales = {}
         x_grouped = {}
+
+        def x_operand(g, batch):
+            lo = X_WORDS_PAD + batch * P
+            return x_codes[g][:, lo:lo + P].bitcast(FP8X4), x_scales[g][:, batch * LINE:batch * LINE + P]
 
         def quantise_x(g):
             x_codes[g] = keep.tile([P, X_WORDS_PAD + BATCHES * P], U32, name="x_codes%d" % g, align_bytes=LINE)
@@ -106,18 +119,14 @@ def tile_readingorderhead_w_kernel(tc, panel_embeddings, W_words, W_scales, b, o
                     out=codes, scales=scales, in_=x_grouped[g][:, batch * GROUP:(batch + 1) * GROUP]
                 )
 
-        def x_operand(g, batch):
-            lo = X_WORDS_PAD + batch * P
-            return x_codes[g][:, lo:lo + P].bitcast(FP8X4), x_scales[g][:, batch * LINE:batch * LINE + P]
-
         for g in range(GROUPS):
-            side, local = g // (GROUPS // 2), g % (GROUPS // 2)
-            bank = psum.tile([P, GROUP], F32, name="x_t%d" % g, tag="bank")
+            piece, local = g // (GROUPS // X_PIECES), g % (GROUPS // X_PIECES)
+            x_t = bank(g, F32, "x_t%d" % g)
             for batch in range(BATCHES):
-                words = x_sb[side][:, batch, :].bitcast(F32)
+                words = x_sb[piece][:, batch, :].bitcast(F32)
                 for u in range(2):
                     nc.tensor.transpose(
-                        bank[:, (2 * batch + u) * P:(2 * batch + u + 1) * P],
+                        x_t[:, (2 * batch + u) * P:(2 * batch + u + 1) * P],
                         words[:, 2 * P * local + u:2 * P * (local + 1):2],
                         ident_f32[:],
                     )
@@ -125,7 +134,7 @@ def tile_readingorderhead_w_kernel(tc, panel_embeddings, W_words, W_scales, b, o
             copy_on(
                 g % 2 == 0,
                 x_grouped[g][:].bitcast(F32).rearrange("p (b i u) -> p b i u", b=BATCHES, u=2),
-                bank[:].rearrange("p (b u i) -> p b i u", b=BATCHES, u=2),
+                x_t[:].rearrange("p (b u i) -> p b i u", b=BATCHES, u=2),
             )
             if g > 0:
                 quantise_x(g - 1)
@@ -138,9 +147,88 @@ def tile_readingorderhead_w_kernel(tc, panel_embeddings, W_words, W_scales, b, o
         bias_f32 = keep.tile([P, 1], F32, name="bias_f32")
         nc.vector.tensor_copy(out=bias_f32[:], in_=bias_bf16[:])
 
+        round_bank = [0,4,0,6,4]
+        score_bank = [2,3]
+        sums = {}
+        xw_bf16 = {}
+        xw_t = {}
+        xw_grouped = {}
         xw_codes = {}
         xw_scales = {}
         scores = []
+
+        def units_of(r):
+            return [(half, batch) for half in range(ROUND_GROUPS[r]) for batch in range(BATCHES)]
+
+        def open_round(r):
+            for i, unit in enumerate(units_of(r)):
+                sums[(r,) + unit] = bank(round_bank[r] + i, F32, "sums%d_%d_%d" % ((r,) + unit))
+
+        def passes(r, g):
+            c = first_group[r] * GROUP // RANGE
+            for (half, batch) in units_of(r):
+                lhsT, lhsT_scale = x_operand(g, batch)
+                lo = (first_group[r] + half) * GROUP - c * RANGE
+                nc.tensor.matmul_mx(
+                    out=sums[(r, half, batch)][:],
+                    lhsT=lhsT,
+                    lhsT_scale=lhsT_scale,
+                    rhs=w_words[(r, g, half)].bitcast(FP8X4),
+                    rhs_scale=w_planes[(c, g // SHARED)][PLANE_ROWS * (g % SHARED):P, lo:lo + GROUP],
+                    start=(g == 0),
+                    stop=(g == GROUPS - 1),
+                )
+
+        def copy_out(r):
+            for i, unit in enumerate(units_of(r)):
+                xw_bf16[(r,) + unit] = work.tile(
+                    [P, GROUP], BF16, name="xw_bf16_%d_%d_%d" % ((r,) + unit), tag="xw_bf16", bufs=8
+                )
+                copy_on(
+                    i % 2 == 1,
+                    xw_bf16[(r,) + unit][:].rearrange("p (u m e) -> p u m e", u=2, e=2),
+                    sums[(r,) + unit][:].rearrange("p (m u e) -> p u m e", u=2, e=2),
+                )
+
+        def transposes(r, split):
+            for (half, batch) in units_of(r):
+                if split:
+                    xw_t[(r, half, batch)] = bank(round_bank[r] + BATCHES * half + batch, F32, "xw_t%d_%d_%d" % (r, half, batch))
+                    target, base = xw_t[(r, half, batch)], 0
+                else:
+                    if batch == 0:
+                        xw_t[(r, half)] = bank(round_bank[r] + BATCHES * half, F32, "xw_t%d_%d" % (r, half))
+                    target, base = xw_t[(r, half)], 2 * batch
+                words = xw_bf16[(r, half, batch)][:].bitcast(F32)
+                for u in range(2):
+                    nc.tensor.transpose(
+                        target[:, (base + u) * P:(base + u + 1) * P], words[:, u * P:(u + 1) * P], ident_f32[:]
+                    )
+
+        def new_group_tiles(r, half):
+            group = first_group[r] + half
+            xw_grouped[group] = work.tile(
+                [P, BATCHES * GROUP], BF16, name="xw_grouped%d" % group, tag="xw_grouped", align_bytes=64
+            )
+            xw_codes[group] = keep.tile([P, BATCHES * P], U32, name="xw_codes%d" % group, align_bytes=64)
+            xw_scales[group] = keep.tile([P, BATCHES * P], U8, name="xw_scales%d" % group, align_bytes=64)
+            return group
+
+        def regroup(r):
+            for half in range(ROUND_GROUPS[r]):
+                group = new_group_tiles(r, half)
+                copy_on(
+                    half % 2 == 1,
+                    xw_grouped[group][:].bitcast(F32).rearrange("p (b i u) -> p b i u", b=BATCHES, u=2),
+                    xw_t[(r, half)][:].rearrange("p (b u i) -> p b i u", b=BATCHES, u=2),
+                )
+
+        def quantise(r):
+            for half in range(ROUND_GROUPS[r]):
+                group = first_group[r] + half
+                nc.vector.quantize_mx(
+                    out=xw_codes[group][:].bitcast(FP8X4), scales=xw_scales[group][:], in_=xw_grouped[group][:]
+                )
 
         def second_matmul(group, batch):
             rhs, rhs_scale = x_operand(group, batch)
@@ -154,72 +242,48 @@ def tile_readingorderhead_w_kernel(tc, panel_embeddings, W_words, W_scales, b, o
                 stop=(group == GROUPS - 1),
             )
 
-        for r in range(ROUNDS):
-            last = r == ROUNDS - 1
-            sums = {}
-            for unit in units:
-                sums[unit] = psum.tile([P, GROUP], F32, name="sums%d_%d_%d" % ((r,) + unit), tag="bank")
-            for g in range(GROUPS):
-                for (half, batch) in units:
-                    lhsT, lhsT_scale = x_operand(g, batch)
-                    nc.tensor.matmul_mx(
-                        out=sums[(half, batch)][:],
-                        lhsT=lhsT,
-                        lhsT_scale=lhsT_scale,
-                        rhs=w_words[(r, g, half)].bitcast(FP8X4),
-                        rhs_scale=w_planes[(r, g // SHARED)][
-                            PLANE_ROWS * (g % SHARED):P, half * GROUP:(half + 1) * GROUP
-                        ],
-                        start=(g == 0),
-                        stop=(g == GROUPS - 1),
-                    )
-            if last:
-                for batch in range(BATCHES):
-                    scores.append(psum.tile([P, GROUP], F32, name="scores%d" % batch, tag="bank"))
+        open_round(0)
+        for g in range(GROUPS):
+            passes(0, g)
+        for r in range(1, rounds):
+            open_round(r)
+            copy_out(r - 1)
+            for g in range(LEAD):
+                passes(r, g)
+            transposes(r - 1, False)
+            regroup(r - 1)
+            passes(r, LEAD)
+            quantise(r - 1)
+            for g in range(LEAD + 1, GROUPS):
+                passes(r, g)
 
-            xw_bf16 = {}
-            for i, unit in enumerate(units):
-                xw_bf16[unit] = work.tile([P, GROUP], BF16, name="xw_bf16_%d_%d_%d" % ((r,) + unit), tag="xw_bf16", bufs=8)
-                copy_on(
-                    i % 2 == 1,
-                    xw_bf16[unit][:].rearrange("p (t m) -> p t m", t=PACK),
-                    sums[unit][:].rearrange("p (m t) -> p t m", t=PACK),
-                )
-            xw_t = {}
-            for unit in units:
-                xw_t[unit] = psum.tile([P, GROUP], BF16, name="xw_t%d_%d_%d" % ((r,) + unit), tag="bank")
-                for t in range(PACK):
-                    nc.tensor.transpose(
-                        xw_t[unit][:, t * P:(t + 1) * P], xw_bf16[unit][:, t * P:(t + 1) * P], ident_bf16[:]
-                    )
-            if last:
-                for group in range(GROUPS - HALVES):
-                    for batch in range(BATCHES):
-                        second_matmul(group, batch)
-            xw_grouped = {}
-            for i, (half, batch) in enumerate(units):
-                if batch == 0:
-                    xw_grouped[half] = work.tile(
-                        [P, BATCHES * GROUP], BF16, name="xw_grouped%d_%d" % (r, half), tag="xw_grouped", align_bytes=64
-                    )
-                copy_on(
-                    i % 2 == 1,
-                    xw_grouped[half][:, batch * GROUP:(batch + 1) * GROUP].rearrange("p (i t) -> p i t", t=PACK),
-                    xw_t[(half, batch)][:].rearrange("p (t i) -> p i t", t=PACK),
-                )
-            for half in range(HALVES):
-                group = r * HALVES + half
-                xw_codes[group] = keep.tile([P, BATCHES * P], U32, name="xw_codes%d" % group, align_bytes=64)
-                xw_scales[group] = keep.tile([P, BATCHES * P], U8, name="xw_scales%d" % group, align_bytes=64)
-                nc.vector.quantize_mx(
-                    out=xw_codes[group][:].bitcast(FP8X4), scales=xw_scales[group][:], in_=xw_grouped[half][:]
-                )
-
-        for group in range(GROUPS - HALVES, GROUPS):
+        last = rounds - 1
+        copy_out(last)
+        for batch in range(BATCHES):
+            scores.append(bank(score_bank[batch], F32, "scores%d" % batch))
+        for group in range(EARLY_FIRST):
             for batch in range(BATCHES):
                 second_matmul(group, batch)
+        transposes(last, True)
+        for group in range(EARLY_FIRST, GROUPS - 1):
+            for batch in range(BATCHES):
+                second_matmul(group, batch)
+        group = new_group_tiles(last, 0)
+        for batch in range(BATCHES):
+            copy_on(
+                batch == 1,
+                xw_grouped[group][:, batch * GROUP:(batch + 1) * GROUP].bitcast(F32).rearrange("p (i u) -> p i u", u=2),
+                xw_t[(last, 0, batch)][:, 0:2 * P].rearrange("p (u i) -> p i u", u=2),
+            )
+        for batch in range(BATCHES):
+            nc.vector.quantize_mx(
+                out=xw_codes[group][:, batch * P:(batch + 1) * P].bitcast(FP8X4),
+                scales=xw_scales[group][:, batch * P:(batch + 1) * P],
+                in_=xw_grouped[group][:, batch * GROUP:(batch + 1) * GROUP],
+            )
         result = keep.tile([P, BATCHES * P], F32, name="result")
         for batch in range(BATCHES):
+            second_matmul(group, batch)
             nc.vector.scalar_tensor_tensor(
                 out=result[:, batch * P:(batch + 1) * P],
                 in0=scores[batch][:, 0:P],

@@ -52,6 +52,11 @@ def tile_readingorderhead_w_kernel(tc, panel_embeddings, W_words, W_scales, b, o
             else:
                 nc.scalar.copy(out=dst, in_=src)
 
+        bias_row = keep.tile([P, 2], BF16, name="bias_row")
+        nc.vector.memset(bias_row[:], 0.0)
+        nc.scalar.dma_start(out=bias_row[0:1, 0:1], in_=b.rearrange("(o n) -> o n", o=1))
+        ones = keep.tile([P, P], BF16, name="ones")
+        nc.vector.memset(ones[:], 1.0)
         w_planes = {}
         for c in range(RANGES):
             for s in range(GROUPS // SHARED):
@@ -59,8 +64,6 @@ def tile_readingorderhead_w_kernel(tc, panel_embeddings, W_words, W_scales, b, o
                 nc.vector.memset(w_planes[(c, s)][:].bitcast(I32), 0)
         ident_f32 = keep.tile([P, P], F32, name="ident_f32")
         make_identity(nc, ident_f32[:])
-        bias_bf16 = keep.tile([P, 1], BF16, name="bias_bf16")
-        nc.scalar.dma_start(out=bias_bf16[:], in_=b.partition_broadcast(P))
 
         x_rows = panel_embeddings.rearrange("b i d -> i b d")
         x_sb = []
@@ -144,8 +147,10 @@ def tile_readingorderhead_w_kernel(tc, panel_embeddings, W_words, W_scales, b, o
         nc.vector.tensor_scalar(
             out=off_diagonal[:], in0=ident_f32[:], scalar1=-1.0, scalar2=1.0, op0=ALU.mult, op1=ALU.add
         )
+        bias_ps = bank(4, F32, "bias_ps")
+        nc.tensor.matmul(bias_ps[:, 0:2], lhsT=ones[:], rhs=bias_row[:], start=True, stop=True)
         bias_f32 = keep.tile([P, 1], F32, name="bias_f32")
-        nc.vector.tensor_copy(out=bias_f32[:], in_=bias_bf16[:])
+        nc.vector.tensor_copy(out=bias_f32[:], in_=bias_ps[:, 0:1])
 
         round_bank = [0,4,0,6,4]
         score_bank = [2,3]

@@ -26,8 +26,7 @@ PLANE_ROWS = QUADRANT // 8
 SHARED = 4
 LINE = 256
 X_WORDS_PAD = 192 // 4
-X_PIECES = 4
-EARLY_FIRST = 4
+EARLY_FIRST = 2
 
 FLOPS = 2 * BATCHES * P * D * D + 2 * BATCHES * P * P * D
 
@@ -65,13 +64,13 @@ def tile_readingorderhead_w_kernel(tc, panel_embeddings, W_words, W_scales, b, o
         ident_f32 = keep.tile([P, P], F32, name="ident_f32")
         make_identity(nc, ident_f32[:])
 
-        x_rows = panel_embeddings.rearrange("b i d -> i b d")
-        x_sb = []
-        for piece in range(X_PIECES):
-            x_sb.append(keep.tile([P, BATCHES, D // X_PIECES], BF16, name="x_sb%d" % piece, align_bytes=LINE))
-            nc.sync.dma_start(
-                out=x_sb[piece][:], in_=x_rows[:, :, piece * (D // X_PIECES):(piece + 1) * (D // X_PIECES)]
-            )
+        x_sb = {}
+        for side in range(2):
+            for batch in range(BATCHES):
+                x_sb[(side, batch)] = keep.tile([P, D // 2], BF16, name="x_sb%d_%d" % (side, batch), align_bytes=LINE)
+                nc.sync.dma_start(
+                    out=x_sb[(side, batch)][:], in_=panel_embeddings[batch, :, side * (D // 2):(side + 1) * (D // 2)]
+                )
         w_words = {}
 
         def load_planes(c, s):
@@ -122,22 +121,26 @@ def tile_readingorderhead_w_kernel(tc, panel_embeddings, W_words, W_scales, b, o
                     out=codes, scales=scales, in_=x_grouped[g][:, batch * GROUP:(batch + 1) * GROUP]
                 )
 
+        x_t = {}
         for g in range(GROUPS):
-            piece, local = g // (GROUPS // X_PIECES), g % (GROUPS // X_PIECES)
-            x_t = bank(g, F32, "x_t%d" % g)
-            for batch in range(BATCHES):
-                words = x_sb[piece][:, batch, :].bitcast(F32)
-                for u in range(2):
-                    nc.tensor.transpose(
-                        x_t[:, (2 * batch + u) * P:(2 * batch + u + 1) * P],
-                        words[:, 2 * P * local + u:2 * P * (local + 1):2],
-                        ident_f32[:],
-                    )
+            x_t[g] = bank(g, F32, "x_t%d" % g)
+        for g in range(GROUPS):
+            side, local = g // (GROUPS // 2), g % (GROUPS // 2)
+            if local == 0:
+                for batch in range(BATCHES):
+                    words = x_sb[(side, batch)][:].bitcast(F32)
+                    for k in range(GROUPS // 2):
+                        for u in range(2):
+                            nc.tensor.transpose(
+                                x_t[g + k][:, (2 * batch + u) * P:(2 * batch + u + 1) * P],
+                                words[:, 2 * P * k + u:2 * P * (k + 1):2],
+                                ident_f32[:],
+                            )
             x_grouped[g] = work.tile([P, BATCHES * GROUP], BF16, name="x_grouped%d" % g, tag="x_grouped", align_bytes=64)
             copy_on(
                 g % 2 == 0,
                 x_grouped[g][:].bitcast(F32).rearrange("p (b i u) -> p b i u", b=BATCHES, u=2),
-                x_t[:].rearrange("p (b u i) -> p b i u", b=BATCHES, u=2),
+                x_t[g][:].rearrange("p (b u i) -> p b i u", b=BATCHES, u=2),
             )
             if g > 0:
                 quantise_x(g - 1)
@@ -297,6 +300,5 @@ def tile_readingorderhead_w_kernel(tc, panel_embeddings, W_words, W_scales, b, o
                 op0=ALU.add,
                 op1=ALU.mult,
             )
-        nc.sync.dma_start(
-            out=out.rearrange("b i j -> i b j"), in_=result[:].rearrange("p (b j) -> p b j", b=BATCHES)
-        )
+            queue = nc.sync if batch == 0 else nc.scalar
+            queue.dma_start(out=out[batch], in_=result[:, batch * P:(batch + 1) * P])

from contextlib import ExitStack

import concourse.mybir as mybir
from concourse.masks import make_identity

F32 = mybir.dt.float32
BF16 = mybir.dt.bfloat16
I32 = mybir.dt.int32
U32 = mybir.dt.uint32
U8 = mybir.dt.uint8
FP8X4 = mybir.dt.float8_e4m3fn_x4
ALU = mybir.AluOpType

P = 128
BATCHES = 2
D = 4096
PACK = 4
GROUP = P * PACK
GROUPS = D // GROUP
RANGE = 2 * GROUP
RANGES = D // RANGE
ROUND_GROUPS = [2,2,2,1,1]
LEAD = 1
QUADRANT = 32
PLANE_ROWS = QUADRANT // 8
SHARED = 4
LINE = 256
X_WORDS_PAD = 192 // 4
EARLY_FIRST = 2

FLOPS = 2 * BATCHES * P * D * D + 2 * BATCHES * P * P * D


def tile_readingorderhead_w_kernel(tc, panel_embeddings, W_words, W_scales, b, out):
    nc = tc.nc
    rounds = len(ROUND_GROUPS)
    first_group = [sum(ROUND_GROUPS[:r]) for r in range(rounds)]

    with ExitStack() as ctx:
        keep = ctx.enter_context(tc.tile_pool(name="keep", bufs=1))
        work = ctx.enter_context(tc.tile_pool(name="work", bufs=4))
        psum = ctx.enter_context(tc.psum_pool(name="psum", bufs=1))
        ctx.enter_context(tc.manual_schedule())

        def bank(k, dtype, name):
            return psum.tile([P, GROUP], dtype, name=name, tag="bank%d" % k)

        def copy_on(on_vector, dst, src):
            if on_vector:
                nc.vector.tensor_copy(out=dst, in_=src)
            else:
                nc.scalar.copy(out=dst, in_=src)

        bias_row = keep.tile([P, 2], BF16, name="bias_row")
        nc.vector.memset(bias_row[:], 0.0)
        nc.scalar.dma_start(out=bias_row[0:1, 0:1], in_=b.rearrange("(o n) -> o n", o=1))
        ones = keep.tile([P, P], BF16, name="ones")
        nc.vector.memset(ones[:], 1.0)
        w_planes = {}
        for c in range(RANGES):
            for s in range(GROUPS // SHARED):
                w_planes[(c, s)] = keep.tile([P, RANGE], U8, name="w_planes%d_%d" % (c, s), align_bytes=LINE)
                nc.vector.memset(w_planes[(c, s)][:].bitcast(I32), 0)
        ident_f32 = keep.tile([P, P], F32, name="ident_f32")
        make_identity(nc, ident_f32[:])

        x_sb = {}
        for side in range(2):
            for batch in range(BATCHES):
                x_sb[(side, batch)] = keep.tile([P, D // 2], BF16, name="x_sb%d_%d" % (side, batch), align_bytes=LINE)
                nc.sync.dma_start(
                    out=x_sb[(side, batch)][:], in_=panel_embeddings[batch, :, side * (D // 2):(side + 1) * (D // 2)]
                )
        w_words = {}

        def load_planes(c, s):
            for quadrant in range(P // QUADRANT):
                nc.sync.dma_start(
                    out=w_planes[(c, s)][QUADRANT * quadrant:QUADRANT * quadrant + SHARED * PLANE_ROWS, :].bitcast(I32),
                    in_=W_scales[
                        s * SHARED:(s + 1) * SHARED,
                        PLANE_ROWS * quadrant:PLANE_ROWS * (quadrant + 1),
                        c * RANGE:(c + 1) * RANGE,
                    ].bitcast(I32),
                )

        def load_w(r, g):
            lo = first_group[r] * GROUP
            width = ROUND_GROUPS[r] * GROUP
            chunk = keep.tile([P, width], U32, name="w_words%d_%d" % (r, g), align_bytes=LINE)
            nc.sync.dma_start(
                out=chunk[:].bitcast(I32),
                in_=W_words[g].rearrange("p n t -> p (n t)")[:, PACK * lo:PACK * (lo + width)].bitcast(I32),
            )
            for half in range(ROUND_GROUPS[r]):
                w_words[(r, g, half)] = chunk[:, half * GROUP:(half + 1) * GROUP]

        planes_loaded = set()
        for r in range(rounds):
            c = first_group[r] * GROUP // RANGE
            for g in range(GROUPS):
                if g % SHARED == 0 and (c, g // SHARED) not in planes_loaded:
                    planes_loaded.add((c, g // SHARED))
                    load_planes(c, g // SHARED)
                load_w(r, g)

        x_codes = {}
        x_scales = {}
        x_grouped = {}

        def x_operand(g, batch):
            lo = X_WORDS_PAD + batch * P
            return x_codes[g][:, lo:lo + P].bitcast(FP8X4), x_scales[g][:, batch * LINE:batch * LINE + P]

        def quantise_x(g):
            x_codes[g] = keep.tile([P, X_WORDS_PAD + BATCHES * P], U32, name="x_codes%d" % g, align_bytes=LINE)
            x_scales[g] = keep.tile([P, BATCHES * LINE], U8, name="x_scales%d" % g, align_bytes=LINE)
            for batch in range(BATCHES):
                codes, scales = x_operand(g, batch)
                nc.vector.quantize_mx(
                    out=codes, scales=scales, in_=x_grouped[g][:, batch * GROUP:(batch + 1) * GROUP]
                )

        x_t = {}
        for g in range(GROUPS):
            x_t[g] = bank(g, F32, "x_t%d" % g)
        for g in range(GROUPS):
            side, local = g // (GROUPS // 2), g % (GROUPS // 2)
            if local == 0:
                for batch in range(BATCHES):
                    words = x_sb[(side, batch)][:].bitcast(F32)
                    for k in range(GROUPS // 2):
                        for u in range(2):
                            nc.tensor.transpose(
                                x_t[g + k][:, (2 * batch + u) * P:(2 * batch + u + 1) * P],
                                words[:, 2 * P * k + u:2 * P * (k + 1):2],
                                ident_f32[:],
                            )
            x_grouped[g] = work.tile([P, BATCHES * GROUP], BF16, name="x_grouped%d" % g, tag="x_grouped", align_bytes=64)
            copy_on(
                g % 2 == 0,
                x_grouped[g][:].bitcast(F32).rearrange("p (b i u) -> p b i u", b=BATCHES, u=2),
                x_t[g][:].rearrange("p (b u i) -> p b i u", b=BATCHES, u=2),
            )
            if g > 0:
                quantise_x(g - 1)
        quantise_x(GROUPS - 1)

        off_diagonal = keep.tile([P, P], F32, name="off_diagonal")
        nc.vector.tensor_scalar(
            out=off_diagonal[:], in0=ident_f32[:], scalar1=-1.0, scalar2=1.0, op0=ALU.mult, op1=ALU.add
        )
        bias_ps = bank(4, F32, "bias_ps")
        nc.tensor.matmul(bias_ps[:, 0:2], lhsT=ones[:], rhs=bias_row[:], start=True, stop=True)
        bias_f32 = keep.tile([P, 1], F32, name="bias_f32")
        nc.vector.tensor_copy(out=bias_f32[:], in_=bias_ps[:, 0:1])

        round_bank = [0,4,0,6,4]
        score_bank = [2,3]
        sums = {}
        xw_bf16 = {}
        xw_t = {}
        xw_grouped = {}
        xw_codes = {}
        xw_scales = {}
        scores = []

        def units_of(r):
            return [(half, batch) for half in range(ROUND_GROUPS[r]) for batch in range(BATCHES)]

        def open_round(r):
            for i, unit in enumerate(units_of(r)):
                sums[(r,) + unit] = bank(round_bank[r] + i, F32, "sums%d_%d_%d" % ((r,) + unit))

        def passes(r, g):
            c = first_group[r] * GROUP // RANGE
            for (half, batch) in units_of(r):
                lhsT, lhsT_scale = x_operand(g, batch)
                lo = (first_group[r] + half) * GROUP - c * RANGE
                nc.tensor.matmul_mx(
                    out=sums[(r, half, batch)][:],
                    lhsT=lhsT,
                    lhsT_scale=lhsT_scale,
                    rhs=w_words[(r, g, half)].bitcast(FP8X4),
                    rhs_scale=w_planes[(c, g // SHARED)][PLANE_ROWS * (g % SHARED):P, lo:lo + GROUP],
                    start=(g == 0),
                    stop=(g == GROUPS - 1),
                )

        def copy_out(r):
            for i, unit in enumerate(units_of(r)):
                xw_bf16[(r,) + unit] = work.tile(
                    [P, GROUP], BF16, name="xw_bf16_%d_%d_%d" % ((r,) + unit), tag="xw_bf16", bufs=8
                )
                copy_on(
                    i % 2 == 1,
                    xw_bf16[(r,) + unit][:].rearrange("p (u m e) -> p u m e", u=2, e=2),
                    sums[(r,) + unit][:].rearrange("p (m u e) -> p u m e", u=2, e=2),
                )

        def transposes(r, split):
            for (half, batch) in units_of(r):
                if split:
                    xw_t[(r, half, batch)] = bank(round_bank[r] + BATCHES * half + batch, F32, "xw_t%d_%d_%d" % (r, half, batch))
                    target, base = xw_t[(r, half, batch)], 0
                else:
                    if batch == 0:
                        xw_t[(r, half)] = bank(round_bank[r] + BATCHES * half, F32, "xw_t%d_%d" % (r, half))
                    target, base = xw_t[(r, half)], 2 * batch
                words = xw_bf16[(r, half, batch)][:].bitcast(F32)
                for u in range(2):
                    nc.tensor.transpose(
                        target[:, (base + u) * P:(base + u + 1) * P], words[:, u * P:(u + 1) * P], ident_f32[:]
                    )

        def new_group_tiles(r, half):
            group = first_group[r] + half
            xw_grouped[group] = work.tile(
                [P, BATCHES * GROUP], BF16, name="xw_grouped%d" % group, tag="xw_grouped", align_bytes=64
            )
            xw_codes[group] = keep.tile([P, BATCHES * P], U32, name="xw_codes%d" % group, align_bytes=64)
            xw_scales[group] = keep.tile([P, BATCHES * P], U8, name="xw_scales%d" % group, align_bytes=64)
            return group

        def regroup(r):
            for half in range(ROUND_GROUPS[r]):
                group = new_group_tiles(r, half)
                copy_on(
                    half % 2 == 1,
                    xw_grouped[group][:].bitcast(F32).rearrange("p (b i u) -> p b i u", b=BATCHES, u=2),
                    xw_t[(r, half)][:].rearrange("p (b u i) -> p b i u", b=BATCHES, u=2),
                )

        def quantise(r):
            for half in range(ROUND_GROUPS[r]):
                group = first_group[r] + half
                nc.vector.quantize_mx(
                    out=xw_codes[group][:].bitcast(FP8X4), scales=xw_scales[group][:], in_=xw_grouped[group][:]
                )

        def second_matmul(group, batch):
            rhs, rhs_scale = x_operand(group, batch)
            nc.tensor.matmul_mx(
                out=scores[batch][:, 0:P],
                lhsT=xw_codes[group][:, batch * P:(batch + 1) * P].bitcast(FP8X4),
                lhsT_scale=xw_scales[group][:, batch * P:(batch + 1) * P],
                rhs=rhs,
                rhs_scale=rhs_scale,
                start=(group == 0),
                stop=(group == GROUPS - 1),
            )

        open_round(0)
        for g in range(GROUPS):
            passes(0, g)
        for r in range(1, rounds):
            open_round(r)
            copy_out(r - 1)
            for g in range(LEAD):
                passes(r, g)
            transposes(r - 1, False)
            regroup(r - 1)
            passes(r, LEAD)
            quantise(r - 1)
            for g in range(LEAD + 1, GROUPS):
                passes(r, g)

        last = rounds - 1
        copy_out(last)
        for batch in range(BATCHES):
            scores.append(bank(score_bank[batch], F32, "scores%d" % batch))
        for group in range(EARLY_FIRST):
            for batch in range(BATCHES):
                second_matmul(group, batch)
        transposes(last, True)
        for group in range(EARLY_FIRST, GROUPS - 1):
            for batch in range(BATCHES):
                second_matmul(group, batch)
        group = new_group_tiles(last, 0)
        for batch in range(BATCHES):
            copy_on(
                batch == 1,
                xw_grouped[group][:, batch * GROUP:(batch + 1) * GROUP].bitcast(F32).rearrange("p (i u) -> p i u", u=2),
                xw_t[(last, 0, batch)][:, 0:2 * P].rearrange("p (u i) -> p i u", u=2),
            )
        for batch in range(BATCHES):
            nc.vector.quantize_mx(
                out=xw_codes[group][:, batch * P:(batch + 1) * P].bitcast(FP8X4),
                scales=xw_scales[group][:, batch * P:(batch + 1) * P],
                in_=xw_grouped[group][:, batch * GROUP:(batch + 1) * GROUP],
            )
        result = keep.tile([P, BATCHES * P], F32, name="result")
        for batch in range(BATCHES):
            second_matmul(group, batch)
            nc.vector.scalar_tensor_tensor(
                out=result[:, batch * P:(batch + 1) * P],
                in0=scores[batch][:, 0:P],
                scalar=bias_f32[:, 0:1],
                in1=off_diagonal[:],
                op0=ALU.add,
                op1=ALU.mult,
            )
            queue = nc.sync if batch == 0 else nc.scalar
            queue.dma_start(out=out[batch], in_=result[:, batch * P:(batch + 1) * P])
